import numpy as np
import ml_dtypes


def mxq(x, axis, fmt="e4m3"):
    dtype, down = {"e4m3": (ml_dtypes.float8_e4m3fn, 7), "e5m2": (ml_dtypes.float8_e5m2, 14)}[fmt]
    v = np.moveaxis(np.asarray(x, np.float32).astype(ml_dtypes.bfloat16).astype(np.float64), axis, -1)
    blocks = v.reshape(v.shape[:-1] + (-1, 32))
    amax = np.abs(blocks).max(-1, keepdims=True)
    byte = np.maximum(np.where(amax > 0, np.frexp(amax)[1] - 1 + 127, 0) - down, 1)
    scale = np.exp2(byte - 127.0)
    codes = (blocks / scale).astype(np.float32).astype(dtype).astype(np.float64)
    return np.moveaxis((codes * scale).reshape(v.shape), -1, axis)


WIDE = False


def mx_kscale(k):
    if not WIDE:
        return np.ones(k)
    levels = np.array([10, -10, 5, -5, 0])
    a = np.random.permutation(np.resize(levels, k // 512 * 4)).reshape(k // 512, 4)
    idx = np.arange(k)
    return np.exp2(a[idx // 512, idx % 128 // 32])


BF16 = ml_dtypes.bfloat16


def bf(x):
    return np.asarray(x, np.float32).astype(BF16)


def f64(x):
    return np.asarray(x).astype(np.float64)


B, N, P, D, H = 8, 512, 4, 128, 2
E = P * D
DH = E // H


def sincos_table(n, e):
    pe = np.zeros((n, e))
    position = np.arange(n, dtype=np.float64)[:, None]
    div_term = np.exp(np.arange(0, e, 2, dtype=np.float64) * -(np.log(10000.0) / e))
    pe[:, 0::2] = np.sin(position * div_term)
    pe[:, 1::2] = np.cos(position * div_term)
    pe = pe - pe.mean()
    return pe / (pe.std() * 10)


def setup_inputs():
    s, t = mx_kscale(E), mx_kscale(E)
    c = 1.0 / np.sqrt(E)
    return {"x": bf(np.random.standard_normal((B, N, P, D)) * s.reshape(P, D)),
            "pos_embed": bf(sincos_table(N, E) * t),
            "W_embed": bf(np.random.standard_normal((E, E)) * c * t[:, None] / s),
            "b_embed": bf(np.random.standard_normal(E) * 0.1 * t),
            "Wq": bf(np.random.standard_normal((E, E)) * c / t),
            "bq": bf(np.random.standard_normal(E) * 0.1),
            "Wk": bf(np.random.standard_normal((E, E)) * c / t),
            "bk": bf(np.random.standard_normal(E) * 0.1),
            "Wv": bf(np.random.standard_normal((E, E)) * c / t),
            "bv": bf(np.random.standard_normal(E) * 0.1)}


def reference(x, pos_embed, W_embed, b_embed, Wq, bq, Wk, bk, Wv, bv):
    xf = f64(x).reshape(B, N, E)
    xe = (mxq(xf, 2, "e4m3") @ mxq(f64(W_embed).T, 0, "e4m3")) + f64(b_embed)
    xe = xe + f64(pos_embed)
    xq = mxq(xe, 2, "e4m3")
    q = ((xq @ mxq(f64(Wq).T, 0, "e4m3")) + f64(bq)).reshape(B, N, H, DH)
    k = ((xq @ mxq(f64(Wk).T, 0, "e4m3")) + f64(bk)).reshape(B, N, H, DH)
    v = ((xq @ mxq(f64(Wv).T, 0, "e4m3")) + f64(bv)).reshape(B, N, H, DH)
    return q, k, v

@@ -1,0 +1,301 @@
+from contextlib import ExitStack
+
+import concourse.mybir as mybir
+from concourse.masks import make_identity
+
+F32 = mybir.dt.float32
+BF16 = mybir.dt.bfloat16
+U32 = mybir.dt.uint32
+U8 = mybir.dt.uint8
+I32 = mybir.dt.int32
+FP8X4 = mybir.dt.float8_e4m3fn_x4
+ADD = mybir.AluOpType.add
+
+P = 128
+E = 512
+GROUPS = 8
+SLABS = 4
+Q_, K_, V_ = 0, 1, 2
+
+FLOPS = 2 * 4096 * 512 * 512 * 4
+
+
+def on_scalar(g, j, o):
+    if o == K_:
+        return True
+    return o == V_ and j == 1 and g < GROUPS - 1
+
+
+def tile_attention_pa_t_kernel(
+    tc, x, pos_embed, W_embed, b_embed, Wq, bq, Wk, bk, Wv, bv, out_0, out_1, out_2
+):
+    nc = tc.nc
+    outs = [out_0, out_1, out_2]
+    weights = [Wq, Wk, Wv]
+    biases = [bq, bk, bv]
+    with ExitStack() as ctx:
+        consts = ctx.enter_context(tc.tile_pool(name="consts", bufs=1))
+        raws = ctx.enter_context(tc.tile_pool(name="raws", bufs=1))
+        work = ctx.enter_context(tc.tile_pool(name="work", bufs=2))
+        stage = ctx.enter_context(tc.tile_pool(name="stage", bufs=4))
+        tp_pool = ctx.enter_context(tc.psum_pool(name="tp", bufs=2))
+        s1_pool = ctx.enter_context(tc.psum_pool(name="s1", bufs=2))
+        s2_pool = ctx.enter_context(tc.psum_pool(name="s2", bufs=4))
+        ctx.enter_context(tc.manual_schedule())
+
+        def bank_of(pool, tag):
+            return pool.tile([P, E], F32, tag=tag, name="bank_" + tag)
+
+        ident = consts.tile([P, P], F32)
+        make_identity(nc, ident[:])
+        ones = consts.tile([P, P], BF16)
+        nc.vector.memset(ones[:], 1.0)
+        rows = consts.tile([P, 3 * E + 256], BF16)
+        nc.vector.memset(rows[:].bitcast(I32), 0)
+
+        nc.scalar.dma_start(
+            out=rows[0:2, 3 * E : 3 * E + 256], in_=b_embed.rearrange("(u w) -> u w", u=2)
+        )
+        we_raw = raws.tile([P, 4 * E], BF16)
+        we_view = W_embed.rearrange("(u m e) k -> u m (e k)", u=2, e=2)
+        for u in range(2):
+            nc.sync.dma_start(out=we_raw[:, 2 * E * u : 2 * E * (u + 1)], in_=we_view[u])
+        x_raw = []
+        for g in range(GROUPS):
+            x_raw.append(raws.tile([P, 4 * E], BF16, name="x_raw%d" % g))
+        x0_view = x[0].rearrange("(c j) a d -> c (j a d)", j=SLABS)
+        for h in range(2):
+            nc.sync.dma_start(
+                out=x_raw[0][:, 2 * E * h : 2 * E * (h + 1)],
+                in_=x0_view[:, 2 * E * h : 2 * E * (h + 1)],
+            )
+        pos_raw = raws.tile([P, 4 * E], BF16)
+        nc.sync.dma_start(
+            out=pos_raw[:], in_=pos_embed.rearrange("(c j) e -> c (j e)", j=SLABS)
+        )
+        w_raw = []
+        for o in range(3):
+            w_raw.append(raws.tile([P, 4 * E], BF16, name="w_raw%d" % o))
+
+        def load_w(o):
+            nc.sync.dma_start(
+                out=w_raw[o][:], in_=weights[o].rearrange("(m s) k -> m (s k)", s=SLABS)
+            )
+
+        load_w(K_)
+        for o in (K_, Q_, V_):
+            nc.sync.dma_start(
+                out=rows[0:1, E * o : E * (o + 1)], in_=biases[o].rearrange("(o n) -> o n", o=1)
+            )
+        load_w(Q_)
+        load_w(V_)
+        for g in range(1, GROUPS):
+            nc.sync.dma_start(
+                out=x_raw[g][:], in_=x[g].rearrange("(c j) a d -> c (j a d)", j=SLABS)
+            )
+
+        def transposes(raw, half, pool, tag):
+            words = raw[:].bitcast(F32)
+            bank = bank_of(pool, tag)
+            for i in range(4):
+                nc.tensor.transpose(
+                    bank[:, P * i : P * (i + 1)],
+                    words[:, E * half + P * i : E * half + P * (i + 1)],
+                    ident[:],
+                )
+            return bank
+
+        def copy_out(engine, out, in_):
+            if engine == "V":
+                nc.vector.tensor_copy(out=out, in_=in_)
+            else:
+                nc.scalar.copy(out=out, in_=in_)
+
+        def flip(raw, interleaved, pool, tag, engines):
+            grouped = work.tile([P, 4 * E], BF16, align_bytes=64, tag="grouped", bufs=4)
+            gwords = grouped[:].bitcast(F32)
+            for half in range(2):
+                bank = transposes(raw, half, pool, tag)
+                if interleaved:
+                    copy_out(
+                        engines[half],
+                        gwords.rearrange("p (m s u) -> p m s u", s=4, u=2)[
+                            :, :, 2 * half : 2 * half + 2, :
+                        ],
+                        bank[:].rearrange("p (s u m) -> p m s u", s=2, u=2),
+                    )
+                else:
+                    copy_out(
+                        engines[half],
+                        gwords.rearrange("p (s m u) -> p s m u", s=4, u=2)[
+                            :, 2 * half : 2 * half + 2, :, :
+                        ],
+                        bank[:].rearrange("p (s u m) -> p s m u", s=2, u=2),
+                    )
+            return grouped
+
+        def quantise(grouped, codes, scales):
+            nc.vector.quantize_mx(out=codes[:].bitcast(FP8X4), scales=scales[:], in_=grouped[:])
+
+        we_codes = consts.tile([P, E], U32, align_bytes=64)
+        we_scales = consts.tile([P, E], U8, align_bytes=64)
+        w_codes = []
+        w_scales = []
+        for o in range(3):
+            w_codes.append(consts.tile([P, E], U32, align_bytes=64, name="w_codes%d" % o))
+            w_scales.append(consts.tile([P, E], U8, align_bytes=64, name="w_scales%d" % o))
+        bias_bc = consts.tile([P, 3 * E], F32)
+        be_pp = consts.tile([P, 4], F32)
+        posbT = consts.tile([P, 4 * E], F32)
+
+        x_grouped = {}
+        x_mx = {}
+        xe_grouped = {}
+        xe_mx = {}
+        s1_acc = {}
+        s2_acc = {}
+        st = {}
+
+        def flip_x(g, pool, tag):
+            x_grouped[g] = flip(x_raw[g], False, pool, tag, ("S", "S"))
+
+        def quant_x(g):
+            x_codes = work.tile([P, E], U32, align_bytes=64, tag="x_codes")
+            x_scales = work.tile([P, E], U8, align_bytes=64, tag="x_scales")
+            quantise(x_grouped[g], x_codes, x_scales)
+            x_mx[g] = (x_codes, x_scales)
+
+        def mm1(g, j, pool, tag):
+            x_codes, x_scales = x_mx[g]
+            acc = bank_of(pool, tag)
+            for t in range(4):
+                nc.tensor.matmul_mx(
+                    out=acc[:, P * t : P * (t + 1)],
+                    lhsT=we_codes[:, P * t : P * (t + 1)].bitcast(FP8X4),
+                    lhsT_scale=we_scales[:, P * t : P * (t + 1)],
+                    rhs=x_codes[:, P * j : P * (j + 1)].bitcast(FP8X4),
+                    rhs_scale=x_scales[:, P * j : P * (j + 1)],
+                    start=True,
+                    stop=True,
+                )
+            s1_acc[j] = acc
+
+        def e1(g, j):
+            if j == 0:
+                gxe = work.tile([P, 4 * E], BF16, align_bytes=64, tag="gxe")
+                xe_grouped[g] = gxe
+            nc.vector.tensor_tensor(
+                out=xe_grouped[g][:, E * j : E * (j + 1)].rearrange("p (c t) -> p c t", t=4),
+                in0=s1_acc[j][:].rearrange("p (t c) -> p c t", t=4),
+                in1=posbT[:, E * j : E * (j + 1)].rearrange("p (c t) -> p c t", t=4),
+                op=ADD,
+            )
+
+        def quant_xe(g):
+            xe_codes = work.tile([P, E], U32, align_bytes=64, tag="xe_codes")
+            xe_scales = work.tile([P, E], U8, align_bytes=64, tag="xe_scales")
+            quantise(xe_grouped[g], xe_codes, xe_scales)
+            xe_mx[g] = (xe_codes, xe_scales)
+
+        def mm2(g, j, o):
+            xe_codes, xe_scales = xe_mx[g]
+            acc = bank_of(s2_pool, "s2")
+            nc.tensor.matmul_mx(
+                out=acc[:],
+                lhsT=xe_codes[:, P * j : P * (j + 1)].bitcast(FP8X4),
+                lhsT_scale=xe_scales[:, P * j : P * (j + 1)],
+                rhs=w_codes[o][:].bitcast(FP8X4),
+                rhs_scale=w_scales[o][:],
+                start=True,
+                stop=True,
+            )
+            s2_acc[o] = acc
+
+        def exit2(g, j, o):
+            dst = st[o][:, E * (j % 2) : E * (j % 2 + 1)]
+            bias = bias_bc[:, E * o : E * (o + 1)]
+            if on_scalar(g, j, o):
+                nc.scalar.copy(out=dst, in_=s2_acc[o][:])
+                nc.gpsimd.tensor_tensor(out=dst, in0=dst, in1=bias, op=ADD)
+            else:
+                nc.vector.tensor_tensor(out=dst, in0=s2_acc[o][:], in1=bias, op=ADD)
+
+        def store(g, o, j0, j1):
+            nc.sync.dma_start(
+                out=outs[o][g].rearrange("(c j) h d -> c (j h d)", j=SLABS)[:, E * j0 : E * j1],
+                in_=st[o][:, E * (j0 % 2) : E * (j0 % 2) + E * (j1 - j0)],
+            )
+
+        we_grouped = flip(we_raw, False, tp_pool, "tp", ("V", "S"))
+        flip_x(0, s1_pool, "s1")
+        be_bank = bank_of(s2_pool, "s2")
+        nc.tensor.transpose(
+            be_bank[:, 0:P], rows[:].bitcast(F32)[:, 3 * E // 2 : 3 * E // 2 + P], ident[:]
+        )
+        nc.scalar.copy(out=be_pp[:], in_=be_bank[:].bitcast(BF16)[:, 0:4])
+        pos_banks = [transposes(pos_raw, half, s2_pool, "s2") for half in range(2)]
+        quantise(we_grouped, we_codes, we_scales)
+        quant_x(0)
+        w_grouped = {}
+        w_grouped[K_] = flip(w_raw[K_], True, tp_pool, "tp", ("S", "S"))
+        mm1_banks = ((s1_pool, "s1"), (s1_pool, "s1"), (s2_pool, "s2"), (s2_pool, "s2"))
+        accs0 = {}
+        for j in range(SLABS):
+            mm1(0, j, mm1_banks[j][0], mm1_banks[j][1])
+            accs0[j] = s1_acc[j]
+        for j in range(SLABS):
+            nc.vector.tensor_tensor(
+                out=posbT[:, E * j : E * (j + 1)].rearrange("p (c u e) -> p c u e", u=2, e=2),
+                in0=pos_banks[j // 2][:]
+                .bitcast(BF16)
+                .rearrange("p (s u c e) -> p s c u e", s=2, u=2, e=2)[:, j % 2],
+                in1=be_pp[:]
+                .rearrange("p (o u e) -> p o u e", o=1, u=2)
+                .to_broadcast([P, P, 2, 2]),
+                op=ADD,
+            )
+        w_grouped[Q_] = flip(w_raw[Q_], True, tp_pool, "tp", ("S", "S"))
+        w_grouped[V_] = flip(w_raw[V_], True, tp_pool, "tp", ("S", "S"))
+        flip_x(1, tp_pool, "tp")
+        for o in (K_, Q_, V_):
+            b_ps = bank_of(s2_pool, "s2")
+            nc.tensor.matmul(
+                out=b_ps[:], lhsT=ones[:], rhs=rows[:, E * o : E * (o + 1)], start=True, stop=True
+            )
+            nc.scalar.copy(out=bias_bc[:, E * o : E * (o + 1)], in_=b_ps[:])
+        for j in range(SLABS):
+            e1(0, j)
+        quantise(w_grouped[K_], w_codes[K_], w_scales[K_])
+        quantise(w_grouped[Q_], w_codes[Q_], w_scales[Q_])
+        quant_xe(0)
+        quantise(w_grouped[V_], w_codes[V_], w_scales[V_])
+        quant_x(1)
+
+        for g in range(GROUPS):
+            last = g == GROUPS - 1
+            for j in range(SLABS):
+                if j % 2 == 0:
+                    for o in range(3):
+                        st[o] = stage.tile([P, 2 * E], F32, name="st%d" % o, tag="st%d" % o)
+                for o in (K_, Q_, V_):
+                    mm2(g, j, o)
+                for o in (K_, Q_, V_):
+                    exit2(g, j, o)
+                if j < 2 and not last:
+                    mm1(g + 1, 2 * j, s1_pool, "s1")
+                    mm1(g + 1, 2 * j + 1, s1_pool, "s1")
+                    e1(g + 1, 2 * j)
+                    e1(g + 1, 2 * j + 1)
+                if j == 0 and g + 2 < GROUPS:
+                    flip_x(g + 2, tp_pool, "tp")
+                if j == 2:
+                    if g + 2 < GROUPS:
+                        quant_x(g + 2)
+                    if not last:
+                        quant_xe(g + 1)
+                if last:
+                    for o in (Q_, V_, K_):
+                        store(g, o, j, j + 1)
+                elif j % 2 == 1:
+                    for o in (Q_, V_, K_):
+                        store(g, o, j - 1, j + 1)

@@ -10,20 +10,56 @@ U8 = mybir.dt.uint8
 I32 = mybir.dt.int32
 FP8X4 = mybir.dt.float8_e4m3fn_x4
 ADD = mybir.AluOpType.add
+IDENTITY = mybir.ActivationFunctionType.Identity
 
 P = 128
 E = 512
+H = 256
 GROUPS = 8
 SLABS = 4
 Q_, K_, V_ = 0, 1, 2
 
 FLOPS = 2 * 4096 * 512 * 512 * 4
 
-
-def on_scalar(g, j, o):
-    if o == K_:
-        return True
-    return o == V_ and j == 1 and g < GROUPS - 1
+K_ON_V = ((7, 3), (7, 2))
+LOAD_ORDER = ('xa', 'pa', 1, 'xb', 'pb', 0, 2)
+PLAN0 = (
+    ("lx", 0, 1), ("tWe", 0, 0), ("tbe", 0, 0), ("tWe", 1, 0), ("xt", 0, 0), ("tposh", 0, 0),
+    ("tW", 2, 0), ("QWe", 0, 0), ("tW", 3, 0), ("Qx", 0, 0), ("s1", 0, 0), ("pos", 1, 0),
+    ("bb", 1, 0), ("pos", 0, 0), ("s1", 1, 0), ("xt", 1, 0), ("e1", 0, 0), ("QW", 1, 0),
+    ("lx", 0, 2), ("tW", 0, 0), ("e1", 1, 0), ("tposh", 1, 0), ("Qxe", 0, 0), ("tW", 1, 0),
+    ("Qx", 1, 0), ("k", 0, 0), ("k", 1, 0), ("xk", 0, 0), ("pos", 2, 0), ("xk", 1, 0),
+    ("QW", 0, 0), ("stk", 0, 0), ("bb", 0, 0), ("pos", 3, 0), ("s1", 3, 0), ("s1", 2, 0),
+    ("bb", 2, 0), ("e1", 2, 0), ("tW", 4, 0), ("q", 1, 0), ("e1", 3, 0), ("xq", 1, 0),
+    ("q", 0, 0), ("tW", 5, 0), ("Qxe", 1, 0), ("bvp", 0, 0), ("xt", 0, 1), ("xq", 0, 0),
+    ("k", 2, 0), ("QW", 2, 0), ("q", 2, 0), ("k", 3, 0), ("xq", 2, 0), ("xk", 2, 0),
+    ("v", 0, 0), ("q", 3, 0), ("lx", 0, 3), ("xq", 3, 0), ("lx", 0, 4), ("xt", 1, 1),
+    ("v", 1, 0), ("xv", 0, 0), ("cm", 0, 0), ("xk", 3, 0), ("xt", 0, 2), ("xt", 1, 2),
+    ("cb", 0, 0), ("v", 2, 0), ("v", 3, 0), ("cm", 1, 0), ("Qx", 2, 1), ("cb", 1, 0),
+    ("s1", 0, 1), ("e1", 0, 1), ("s1", 2, 1), ("e1", 2, 1), ("s1", 1, 1), ("s1", 3, 1),
+    ("Qx", 2, 2), ("stk", 1, 0), ("stq", 0, 0), ("ct", 0, 0), ("e1", 1, 1), ("stv", 0, 0),
+    ("e1", 3, 1), ("s1", 0, 2), ("stq", 1, 0), ("xv", 1, 0), ("ct", 1, 0), ("s1", 1, 2),
+    ("stv", 1, 0), ("Qxe", 2, 1), ("e1", 0, 2), ("e1", 1, 2),
+)
+PLAN = (
+    ("k", 0, 0), ("q", 0, 0), ("cm", 0, 0), ("xq", 0, 0), ("lx", 0, 4), ("s1", 2, 1),
+    ("v", 0, 0), ("xk", 0, 0), ("cm", 1, 0), ("cb", 0, 0), ("s1", 3, 1), ("k", 1, 0),
+    ("cb", 1, 0), ("xk", 1, 0), ("e1", 2, 1), ("q", 1, 0), ("v", 1, 0), ("e1", 3, 1),
+    ("xq", 1, 0), ("xt", 0, 2), ("stq", 0, 0), ("xt", 1, 2), ("q", 2, 0), ("k", 2, 0),
+    ("xv", 0, 0), ("stk", 0, 0), ("ct", 0, 0), ("k", 3, 0), ("q", 3, 0), ("xk", 3, 0),
+    ("v", 2, 0), ("stv", 0, 0), ("xq", 2, 0), ("v", 3, 0), ("xk", 2, 0), ("Qxe", 2, 1),
+    ("Qx", 2, 2), ("xq", 3, 0), ("ct", 1, 0), ("stq", 1, 0), ("s1", 0, 2), ("xv", 1, 0),
+    ("s1", 1, 2), ("e1", 0, 2), ("stv", 1, 0), ("e1", 1, 2), ("stk", 1, 0),
+)
+PLAN_LAST = (
+    ("cm", 0, 0), ("cb", 0, 0), ("k", 0, 0), ("cm", 1, 0), ("cb", 1, 0), ("xk", 0, 0),
+    ("v", 0, 0), ("k", 1, 0), ("ct", 0, 0), ("ct", 1, 0), ("q", 1, 0), ("v", 1, 0),
+    ("svh", 1, 0), ("xk", 1, 0), ("xq", 1, 0), ("q", 0, 0), ("q", 3, 0), ("xq", 0, 0),
+    ("v", 2, 0), ("xv", 0, 0), ("xq", 3, 0), ("stq", 0, 0), ("v", 3, 0), ("xv", 1, 0),
+    ("k", 3, 0), ("k", 2, 0), ("q", 2, 0), ("xq", 2, 0), ("stk", 0, 0), ("xk", 3, 0),
+    ("sq", 3, 0), ("sq", 2, 0), ("xk", 2, 0), ("sk", 3, 0), ("svl", 1, 0), ("sk", 2, 0),
+    ("stv", 0, 0),
+)
 
 
 def tile_attention_pa_t_kernel(
@@ -40,7 +76,8 @@ def tile_attention_pa_t_kernel(
         stage = ctx.enter_context(tc.tile_pool(name="stage", bufs=4))
         tp_pool = ctx.enter_context(tc.psum_pool(name="tp", bufs=2))
         s1_pool = ctx.enter_context(tc.psum_pool(name="s1", bufs=2))
-        s2_pool = ctx.enter_context(tc.psum_pool(name="s2", bufs=4))
+        s2_pool = ctx.enter_context(tc.psum_pool(name="s2", bufs=3))
+        vb_pool = ctx.enter_context(tc.psum_pool(name="vb", bufs=1))
         ctx.enter_context(tc.manual_schedule())
 
         def bank_of(pool, tag):
@@ -48,14 +85,14 @@ def tile_attention_pa_t_kernel(
 
         ident = consts.tile([P, P], F32)
         make_identity(nc, ident[:])
+        be_rows = consts.tile([P, H], BF16)
+        nc.vector.memset(be_rows[:].bitcast(I32), 0)
         ones = consts.tile([P, P], BF16)
         nc.vector.memset(ones[:], 1.0)
-        rows = consts.tile([P, 3 * E + 256], BF16)
+        rows = consts.tile([P, 3 * E], BF16)
         nc.vector.memset(rows[:].bitcast(I32), 0)
 
-        nc.scalar.dma_start(
-            out=rows[0:2, 3 * E : 3 * E + 256], in_=b_embed.rearrange("(u w) -> u w", u=2)
-        )
+        nc.sync.dma_start(out=be_rows[0:2, :], in_=b_embed.rearrange("(u w) -> u w", u=2))
         we_raw = raws.tile([P, 4 * E], BF16)
         we_view = W_embed.rearrange("(u m e) k -> u m (e k)", u=2, e=2)
         for u in range(2):
@@ -64,78 +101,34 @@ def tile_attention_pa_t_kernel(
         for g in range(GROUPS):
             x_raw.append(raws.tile([P, 4 * E], BF16, name="x_raw%d" % g))
         x0_view = x[0].rearrange("(c j) a d -> c (j a d)", j=SLABS)
-        for h in range(2):
-            nc.sync.dma_start(
-                out=x_raw[0][:, 2 * E * h : 2 * E * (h + 1)],
-                in_=x0_view[:, 2 * E * h : 2 * E * (h + 1)],
-            )
         pos_raw = raws.tile([P, 4 * E], BF16)
-        nc.sync.dma_start(
-            out=pos_raw[:], in_=pos_embed.rearrange("(c j) e -> c (j e)", j=SLABS)
-        )
+        pos_view = pos_embed.rearrange("(c j) e -> c (j e)", j=SLABS)
         w_raw = []
         for o in range(3):
             w_raw.append(raws.tile([P, 4 * E], BF16, name="w_raw%d" % o))
 
-        def load_w(o):
+        def load_half(dst, view, h):
             nc.sync.dma_start(
-                out=w_raw[o][:], in_=weights[o].rearrange("(m s) k -> m (s k)", s=SLABS)
+                out=dst[:, 2 * E * h : 2 * E * (h + 1)], in_=view[:, 2 * E * h : 2 * E * (h + 1)]
             )
 
-        load_w(K_)
-        for o in (K_, Q_, V_):
-            nc.sync.dma_start(
-                out=rows[0:1, E * o : E * (o + 1)], in_=biases[o].rearrange("(o n) -> o n", o=1)
-            )
-        load_w(Q_)
-        load_w(V_)
-        for g in range(1, GROUPS):
-            nc.sync.dma_start(
-                out=x_raw[g][:], in_=x[g].rearrange("(c j) a d -> c (j a d)", j=SLABS)
-            )
-
-        def transposes(raw, half, pool, tag):
-            words = raw[:].bitcast(F32)
-            bank = bank_of(pool, tag)
-            for i in range(4):
-                nc.tensor.transpose(
-                    bank[:, P * i : P * (i + 1)],
-                    words[:, E * half + P * i : E * half + P * (i + 1)],
-                    ident[:],
-                )
-            return bank
-
-        def copy_out(engine, out, in_):
-            if engine == "V":
-                nc.vector.tensor_copy(out=out, in_=in_)
+        for what in LOAD_ORDER:
+            if what == "xa":
+                load_half(x_raw[0], x0_view, 0)
+            elif what == "xb":
+                load_half(x_raw[0], x0_view, 1)
+            elif what == "pa":
+                load_half(pos_raw, pos_view, 0)
+            elif what == "pb":
+                load_half(pos_raw, pos_view, 1)
             else:
-                nc.scalar.copy(out=out, in_=in_)
-
-        def flip(raw, interleaved, pool, tag, engines):
-            grouped = work.tile([P, 4 * E], BF16, align_bytes=64, tag="grouped", bufs=4)
-            gwords = grouped[:].bitcast(F32)
-            for half in range(2):
-                bank = transposes(raw, half, pool, tag)
-                if interleaved:
-                    copy_out(
-                        engines[half],
-                        gwords.rearrange("p (m s u) -> p m s u", s=4, u=2)[
-                            :, :, 2 * half : 2 * half + 2, :
-                        ],
-                        bank[:].rearrange("p (s u m) -> p m s u", s=2, u=2),
-                    )
-                else:
-                    copy_out(
-                        engines[half],
-                        gwords.rearrange("p (s m u) -> p s m u", s=4, u=2)[
-                            :, 2 * half : 2 * half + 2, :, :
-                        ],
-                        bank[:].rearrange("p (s u m) -> p s m u", s=2, u=2),
-                    )
-            return grouped
-
-        def quantise(grouped, codes, scales):
-            nc.vector.quantize_mx(out=codes[:].bitcast(FP8X4), scales=scales[:], in_=grouped[:])
+                nc.sync.dma_start(
+                    out=w_raw[what][:], in_=weights[what].rearrange("(m s) k -> m (s k)", s=SLABS)
+                )
+                nc.sync.dma_start(
+                    out=rows[0:1, E * what : E * (what + 1)],
+                    in_=biases[what].rearrange("(o n) -> o n", o=1),
+                )
 
         we_codes = consts.tile([P, E], U32, align_bytes=64)
         we_scales = consts.tile([P, E], U8, align_bytes=64)
@@ -146,156 +139,288 @@ def tile_attention_pa_t_kernel(
             w_scales.append(consts.tile([P, E], U8, align_bytes=64, name="w_scales%d" % o))
         bias_bc = consts.tile([P, 3 * E], F32)
         be_pp = consts.tile([P, 4], F32)
+        bv_pp = consts.tile([P, 2], F32)
         posbT = consts.tile([P, 4 * E], F32)
 
-        x_grouped = {}
-        x_mx = {}
-        xe_grouped = {}
-        xe_mx = {}
-        s1_acc = {}
-        s2_acc = {}
-        st = {}
+        live = {}
+        done = set()
 
-        def flip_x(g, pool, tag):
-            x_grouped[g] = flip(x_raw[g], False, pool, tag, ("S", "S"))
+        def need(*keys):
+            for key in keys:
+                assert key in done, key
 
-        def quant_x(g):
-            x_codes = work.tile([P, E], U32, align_bytes=64, tag="x_codes")
-            x_scales = work.tile([P, E], U8, align_bytes=64, tag="x_scales")
-            quantise(x_grouped[g], x_codes, x_scales)
-            x_mx[g] = (x_codes, x_scales)
+        def new_grouped():
+            grouped = work.tile([P, 4 * E], BF16, align_bytes=64, tag="grouped", bufs=4)
+            return grouped
 
-        def mm1(g, j, pool, tag):
-            x_codes, x_scales = x_mx[g]
-            acc = bank_of(pool, tag)
-            for t in range(4):
-                nc.tensor.matmul_mx(
-                    out=acc[:, P * t : P * (t + 1)],
-                    lhsT=we_codes[:, P * t : P * (t + 1)].bitcast(FP8X4),
-                    lhsT_scale=we_scales[:, P * t : P * (t + 1)],
-                    rhs=x_codes[:, P * j : P * (j + 1)].bitcast(FP8X4),
-                    rhs_scale=x_scales[:, P * j : P * (j + 1)],
-                    start=True,
-                    stop=True,
+        def flip_half(raw, grouped, half, interleaved, pool, tag, engine):
+            words = raw[:].bitcast(F32)
+            bank = bank_of(pool, tag)
+            for i in range(4):
+                nc.tensor.transpose(
+                    bank[:, P * i : P * (i + 1)],
+                    words[:, E * half + P * i : E * half + P * (i + 1)],
+                    ident[:],
                 )
-            s1_acc[j] = acc
+            gwords = grouped[:].bitcast(F32)
+            if interleaved:
+                dst = gwords.rearrange("p (m s u) -> p m s u", s=4, u=2)[
+                    :, :, 2 * half : 2 * half + 2, :
+                ]
+                src = bank[:].rearrange("p (s u m) -> p m s u", s=2, u=2)
+            else:
+                dst = gwords.rearrange("p (s m u) -> p s m u", s=4, u=2)[
+                    :, 2 * half : 2 * half + 2, :, :
+                ]
+                src = bank[:].rearrange("p (s u m) -> p s m u", s=2, u=2)
+            if engine == "V":
+                nc.vector.tensor_copy(out=dst, in_=src)
+            else:
+                nc.scalar.copy(out=dst, in_=src)
 
-        def e1(g, j):
-            if j == 0:
-                gxe = work.tile([P, 4 * E], BF16, align_bytes=64, tag="gxe")
-                xe_grouped[g] = gxe
-            nc.vector.tensor_tensor(
-                out=xe_grouped[g][:, E * j : E * (j + 1)].rearrange("p (c t) -> p c t", t=4),
-                in0=s1_acc[j][:].rearrange("p (t c) -> p c t", t=4),
-                in1=posbT[:, E * j : E * (j + 1)].rearrange("p (c t) -> p c t", t=4),
-                op=ADD,
+        def quantise(grouped, codes, scales, c0, c1):
+            nc.vector.quantize_mx(
+                out=codes[:, c0:c1].bitcast(FP8X4),
+                scales=scales[:, c0:c1],
+                in_=grouped[:, 4 * c0 : 4 * c1],
             )
 
-        def quant_xe(g):
-            xe_codes = work.tile([P, E], U32, align_bytes=64, tag="xe_codes")
-            xe_scales = work.tile([P, E], U8, align_bytes=64, tag="xe_scales")
-            quantise(xe_grouped[g], xe_codes, xe_scales)
-            xe_mx[g] = (xe_codes, xe_scales)
+        def mx_pair(tag):
+            codes = work.tile([P, E], U32, align_bytes=64, tag=tag + "_codes", name=tag + "_codes")
+            scales = work.tile([P, E], U8, align_bytes=64, tag=tag + "_scales", name=tag + "_scales")
+            return (codes, scales)
 
-        def mm2(g, j, o):
-            xe_codes, xe_scales = xe_mx[g]
-            acc = bank_of(s2_pool, "s2")
+        def st_tile(g, o, pair):
+            key = ("st", g, o, pair)
+            if key not in live:
+                live[key] = stage.tile([P, 2 * E], F32, name="st%d" % o, tag="st%d" % o)
+            return live[key]
+
+        def mx(out, lhsT, l0, l1, rhs, r0, r1):
             nc.tensor.matmul_mx(
-                out=acc[:],
-                lhsT=xe_codes[:, P * j : P * (j + 1)].bitcast(FP8X4),
-                lhsT_scale=xe_scales[:, P * j : P * (j + 1)],
-                rhs=w_codes[o][:].bitcast(FP8X4),
-                rhs_scale=w_scales[o][:],
+                out=out,
+                lhsT=lhsT[0][:, l0:l1].bitcast(FP8X4),
+                lhsT_scale=lhsT[1][:, l0:l1],
+                rhs=rhs[0][:, r0:r1].bitcast(FP8X4),
+                rhs_scale=rhs[1][:, r0:r1],
                 start=True,
                 stop=True,
             )
-            s2_acc[o] = acc
 
-        def exit2(g, j, o):
-            dst = st[o][:, E * (j % 2) : E * (j % 2 + 1)]
-            bias = bias_bc[:, E * o : E * (o + 1)]
-            if on_scalar(g, j, o):
-                nc.scalar.copy(out=dst, in_=s2_acc[o][:])
-                nc.gpsimd.tensor_tensor(out=dst, in0=dst, in1=bias, op=ADD)
+        def do(op, a, g):
+            if g >= GROUPS:
+                return
+            key = (op, a, g)
+            assert key not in done, key
+            pair = a // 2
+            if op == "lx":
+                nc.sync.dma_start(
+                    out=x_raw[g][:], in_=x[g].rearrange("(c j) a d -> c (j a d)", j=SLABS)
+                )
+            elif op == "tWe":
+                if a == 0:
+                    live["gwe"] = new_grouped()
+                flip_half(we_raw, live["gwe"], a, False, tp_pool, "tp", "VS"[a])
+            elif op == "QWe":
+                need(("tWe", 0, 0), ("tWe", 1, 0))
+                quantise(live["gwe"], we_codes, we_scales, 0, E)
+            elif op == "tbe":
+                bank = bank_of(s2_pool, "s2")
+                nc.tensor.transpose(bank[:, 0:P], be_rows[:].bitcast(F32), ident[:])
+                nc.scalar.copy(out=be_pp[:], in_=bank[:].bitcast(BF16)[:, 0:4])
+            elif op == "tposh":
+                words = pos_raw[:].bitcast(F32)
+                bank = bank_of((s2_pool, vb_pool)[a], ("s2", "vb")[a])
+                for i in range(4):
+                    nc.tensor.transpose(
+                        bank[:, P * i : P * (i + 1)],
+                        words[:, E * a + P * i : E * a + P * (i + 1)],
+                        ident[:],
+                    )
+                live[("posbank", a)] = bank
+            elif op == "pos":
+                need(("tposh", pair, 0), ("tbe", 0, 0))
+                nc.vector.tensor_tensor(
+                    out=posbT[:, E * a : E * (a + 1)].rearrange("p (c u e) -> p c u e", u=2, e=2),
+                    in0=live[("posbank", pair)][:]
+                    .bitcast(BF16)
+                    .rearrange("p (s u c e) -> p s c u e", s=2, u=2, e=2)[:, a % 2],
+                    in1=be_pp[:]
+                    .rearrange("p (o u e) -> p o u e", o=1, u=2)
+                    .to_broadcast([P, P, 2, 2]),
+                    op=ADD,
+                )
+            elif op == "tW":
+                if a % 2 == 0:
+                    live[("gw", pair)] = new_grouped()
+                else:
+                    need(("tW", a - 1, 0))
+                flip_half(w_raw[pair], live[("gw", pair)], a % 2, True, tp_pool, "tp", "S")
+            elif op == "QW":
+                need(("tW", 2 * a, 0), ("tW", 2 * a + 1, 0))
+                quantise(live[("gw", a)], w_codes[a], w_scales[a], 0, E)
+            elif op == "bb":
+                bank = bank_of(s2_pool, "s2")
+                nc.tensor.matmul(
+                    out=bank[:], lhsT=ones[:], rhs=rows[:, E * a : E * (a + 1)], start=True, stop=True
+                )
+                nc.scalar.copy(out=bias_bc[:, E * a : E * (a + 1)], in_=bank[:])
+            elif op == "bvp":
+                need(("bb", V_, 0))
+                bank = bank_of(s2_pool, "s2")
+                for i in range(2):
+                    nc.tensor.transpose(
+                        bank[:, P * i : P * (i + 1)],
+                        bias_bc[:, E * V_ + H + P * i : E * V_ + H + P * (i + 1)],
+                        ident[:],
+                    )
+                nc.scalar.copy(
+                    out=bv_pp[:].unsqueeze(2),
+                    in_=bank[:].rearrange("p (i c) -> p i c", c=P)[:, 0:2, 0:1],
+                )
+            elif op == "xt":
+                if g > 0:
+                    need(("lx", 0, g))
+                if a == 0:
+                    live[("gx", g)] = new_grouped()
+                else:
+                    need(("xt", 0, g))
+                flip_half(x_raw[g], live[("gx", g)], a, False, tp_pool, "tp", "S")
+            elif op == "Qx":
+                if a in (0, 2):
+                    live[("x", g)] = mx_pair("x")
+                if a == 1:
+                    need(("Qx", 0, g))
+                need(*[("xt", h, g) for h in ((0, 1) if a == 2 else (a,))])
+                c0, c1 = ((0, H), (H, E), (0, E))[a]
+                quantise(live[("gx", g)], live[("x", g)][0], live[("x", g)][1], c0, c1)
+                if a == 2:
+                    done.add(("Qx", 0, g))
+                    done.add(("Qx", 1, g))
+            elif op == "s1":
+                need(("Qx", pair, g), ("QWe", 0, 0))
+                bank = bank_of(s1_pool, "s1")
+                for t in range(4):
+                    mx(bank[:, P * t : P * (t + 1)], (we_codes, we_scales), P * t, P * (t + 1),
+                       live[("x", g)], P * a, P * (a + 1))
+                live[("s1", g, a)] = bank
+            elif op == "e1":
+                need(("s1", a, g), ("pos", a, 0))
+                if ("gxe", g) not in live:
+                    gxe = work.tile([P, 4 * E], BF16, align_bytes=64, tag="gxe")
+                    live[("gxe", g)] = gxe
+                nc.vector.tensor_tensor(
+                    out=live[("gxe", g)][:, E * a : E * (a + 1)].rearrange("p (c t) -> p c t", t=4),
+                    in0=live[("s1", g, a)][:].rearrange("p (t c) -> p c t", t=4),
+                    in1=posbT[:, E * a : E * (a + 1)].rearrange("p (c t) -> p c t", t=4),
+                    op=ADD,
+                )
+            elif op == "Qxe":
+                if a in (0, 2):
+                    live[("xe", g)] = mx_pair("xe")
+                if a == 1:
+                    need(("Qxe", 0, g))
+                need(*[("e1", j, g) for j in ((0, 1), (2, 3), (0, 1, 2, 3))[a]])
+                c0, c1 = ((0, H), (H, E), (0, E))[a]
+                quantise(live[("gxe", g)], live[("xe", g)][0], live[("xe", g)][1], c0, c1)
+                if a == 2:
+                    done.add(("Qxe", 0, g))
+                    done.add(("Qxe", 1, g))
+            elif op in ("k", "q"):
+                o = K_ if op == "k" else Q_
+                need(("Qxe", pair, g), ("QW", o, 0))
+                bank = bank_of(s2_pool, "s2")
+                mx(bank[:], live[("xe", g)], P * a, P * (a + 1), (w_codes[o], w_scales[o]), 0, E)
+                live[(op, g, a)] = bank
+            elif op in ("xk", "xq"):
+                o = K_ if op == "xk" else Q_
+                need((op[1], a, g), ("bb", o, 0))
+                dst = st_tile(g, o, pair)[:, E * (a % 2) : E * (a % 2 + 1)]
+                bias = bias_bc[:, E * o : E * (o + 1)]
+                bank = live[(op[1], g, a)]
+                if o == K_ and (g, a) not in K_ON_V:
+                    nc.scalar.copy(out=dst, in_=bank[:])
+                    nc.gpsimd.tensor_tensor(out=dst, in0=dst, in1=bias, op=ADD)
+                else:
+                    nc.vector.tensor_tensor(out=dst, in0=bank[:], in1=bias, op=ADD)
+            elif op == "v":
+                need(("Qxe", pair, g), ("QW", V_, 0))
+                if a % 2 == 0:
+                    live[("v", g, pair)] = bank_of(vb_pool, "vb")
+                else:
+                    need(("v", a - 1, g))
+                mx(live[("v", g, pair)][:, H * (a % 2) : H * (a % 2 + 1)], live[("xe", g)],
+                   P * a, P * (a + 1), (w_codes[V_], w_scales[V_]), 0, H)
+            elif op == "xv":
+                need(("v", 2 * a, g), ("v", 2 * a + 1, g), ("bb", V_, 0))
+                nc.vector.tensor_tensor(
+                    out=st_tile(g, V_, a)[:].rearrange("c (j e) -> c j e", j=2)[:, :, 0:H],
+                    in0=live[("v", g, a)][:].rearrange("c (j e) -> c j e", j=2),
+                    in1=bias_bc[:, E * V_ : E * V_ + H].unsqueeze(1).to_broadcast([P, 2, H]),
+                    op=ADD,
+                )
+            elif op == "cm":
+                need(("Qxe", 0, g), ("Qxe", 1, g), ("QW", V_, 0))
+                bank = bank_of(s2_pool, "s2")
+                mx(bank[:], (w_codes[V_], w_scales[V_]), H + P * a, H + P * (a + 1), live[("xe", g)], 0, E)
+                live[("cm", g, a)] = bank
+            elif op == "cb":
+                need(("cm", a, g), ("bvp", 0, 0))
+                tmp = work.tile([P, E], F32, tag="c_tmp", bufs=4)
+                nc.scalar.activation(
+                    out=tmp[:], in_=live[("cm", g, a)][:], func=IDENTITY, bias=bv_pp[:, a : a + 1]
+                )
+                live[("cb", g, a)] = tmp
+            elif op == "ct":
+                need(("cb", 0, g), ("cb", 1, g))
+                bank = bank_of(tp_pool, "tp")
+                for j2 in range(2):
+                    for i in range(2):
+                        nc.tensor.transpose(
+                            bank[:, P * (2 * j2 + i) : P * (2 * j2 + i + 1)],
+                            live[("cb", g, i)][:, P * (2 * a + j2) : P * (2 * a + j2 + 1)],
+                            ident[:],
+                        )
+                nc.scalar.copy(
+                    out=st_tile(g, V_, a)[:].rearrange("c (j e) -> c j e", j=2)[:, :, H:E],
+                    in_=bank[:].rearrange("c (j e) -> c j e", j=2),
+                )
+            elif op in ("stq", "stk", "stv"):
+                o = {"stq": Q_, "stk": K_, "stv": V_}[op]
+                if o == V_:
+                    need(("xv", a, g), ("ct", a, g))
+                else:
+                    need(("x" + op[2], 2 * a, g), ("x" + op[2], 2 * a + 1, g))
+                nc.sync.dma_start(
+                    out=outs[o][g].rearrange("(c j) h d -> c (j h d)", j=SLABS)[
+                        :, 2 * E * a : 2 * E * (a + 1)
+                    ],
+                    in_=live[("st", g, o, a)][:],
+                )
+            elif op in ("sq", "sk"):
+                o = {"sq": Q_, "sk": K_}[op]
+                need(("x" + op[1], a, g))
+                nc.sync.dma_start(
+                    out=outs[o][g].rearrange("(c j) h d -> c (j h d)", j=SLABS)[:, E * a : E * (a + 1)],
+                    in_=live[("st", g, o, pair)][:, E * (a % 2) : E * (a % 2 + 1)],
+                )
+            elif op in ("svl", "svh"):
+                need(("xv", a, g) if op == "svl" else ("ct", a, g))
+                e0 = 0 if op == "svl" else H
+                nc.sync.dma_start(
+                    out=outs[V_][g].rearrange("(c j) h d -> c j (h d)", j=SLABS)[
+                        :, 2 * a : 2 * a + 2, e0 : e0 + H
+                    ],
+                    in_=live[("st", g, V_, a)][:].rearrange("c (j e) -> c j e", j=2)[:, :, e0 : e0 + H],
+                )
             else:
-                nc.vector.tensor_tensor(out=dst, in0=s2_acc[o][:], in1=bias, op=ADD)
+                assert False, op
+            done.add(key)
 
-        def store(g, o, j0, j1):
-            nc.sync.dma_start(
-                out=outs[o][g].rearrange("(c j) h d -> c (j h d)", j=SLABS)[:, E * j0 : E * j1],
-                in_=st[o][:, E * (j0 % 2) : E * (j0 % 2) + E * (j1 - j0)],
-            )
-
-        we_grouped = flip(we_raw, False, tp_pool, "tp", ("V", "S"))
-        flip_x(0, s1_pool, "s1")
-        be_bank = bank_of(s2_pool, "s2")
-        nc.tensor.transpose(
-            be_bank[:, 0:P], rows[:].bitcast(F32)[:, 3 * E // 2 : 3 * E // 2 + P], ident[:]
-        )
-        nc.scalar.copy(out=be_pp[:], in_=be_bank[:].bitcast(BF16)[:, 0:4])
-        pos_banks = [transposes(pos_raw, half, s2_pool, "s2") for half in range(2)]
-        quantise(we_grouped, we_codes, we_scales)
-        quant_x(0)
-        w_grouped = {}
-        w_grouped[K_] = flip(w_raw[K_], True, tp_pool, "tp", ("S", "S"))
-        mm1_banks = ((s1_pool, "s1"), (s1_pool, "s1"), (s2_pool, "s2"), (s2_pool, "s2"))
-        accs0 = {}
-        for j in range(SLABS):
-            mm1(0, j, mm1_banks[j][0], mm1_banks[j][1])
-            accs0[j] = s1_acc[j]
-        for j in range(SLABS):
-            nc.vector.tensor_tensor(
-                out=posbT[:, E * j : E * (j + 1)].rearrange("p (c u e) -> p c u e", u=2, e=2),
-                in0=pos_banks[j // 2][:]
-                .bitcast(BF16)
-                .rearrange("p (s u c e) -> p s c u e", s=2, u=2, e=2)[:, j % 2],
-                in1=be_pp[:]
-                .rearrange("p (o u e) -> p o u e", o=1, u=2)
-                .to_broadcast([P, P, 2, 2]),
-                op=ADD,
-            )
-        w_grouped[Q_] = flip(w_raw[Q_], True, tp_pool, "tp", ("S", "S"))
-        w_grouped[V_] = flip(w_raw[V_], True, tp_pool, "tp", ("S", "S"))
-        flip_x(1, tp_pool, "tp")
-        for o in (K_, Q_, V_):
-            b_ps = bank_of(s2_pool, "s2")
-            nc.tensor.matmul(
-                out=b_ps[:], lhsT=ones[:], rhs=rows[:, E * o : E * (o + 1)], start=True, stop=True
-            )
-            nc.scalar.copy(out=bias_bc[:, E * o : E * (o + 1)], in_=b_ps[:])
-        for j in range(SLABS):
-            e1(0, j)
-        quantise(w_grouped[K_], w_codes[K_], w_scales[K_])
-        quantise(w_grouped[Q_], w_codes[Q_], w_scales[Q_])
-        quant_xe(0)
-        quantise(w_grouped[V_], w_codes[V_], w_scales[V_])
-        quant_x(1)
-
-        for g in range(GROUPS):
-            last = g == GROUPS - 1
-            for j in range(SLABS):
-                if j % 2 == 0:
-                    for o in range(3):
-                        st[o] = stage.tile([P, 2 * E], F32, name="st%d" % o, tag="st%d" % o)
-                for o in (K_, Q_, V_):
-                    mm2(g, j, o)
-                for o in (K_, Q_, V_):
-                    exit2(g, j, o)
-                if j < 2 and not last:
-                    mm1(g + 1, 2 * j, s1_pool, "s1")
-                    mm1(g + 1, 2 * j + 1, s1_pool, "s1")
-                    e1(g + 1, 2 * j)
-                    e1(g + 1, 2 * j + 1)
-                if j == 0 and g + 2 < GROUPS:
-                    flip_x(g + 2, tp_pool, "tp")
-                if j == 2:
-                    if g + 2 < GROUPS:
-                        quant_x(g + 2)
-                    if not last:
-                        quant_xe(g + 1)
-                if last:
-                    for o in (Q_, V_, K_):
-                        store(g, o, j, j + 1)
-                elif j % 2 == 1:
-                    for o in (Q_, V_, K_):
-                        store(g, o, j - 1, j + 1)
+        for op, a, dg in PLAN0:
+            do(op, a, dg)
+        for g in range(1, GROUPS - 1):
+            for op, a, dg in PLAN:
+                do(op, a, g + dg)
+        for op, a, dg in PLAN_LAST:
+            do(op, a, GROUPS - 1 + dg)

@@ -14,52 +14,12 @@ IDENTITY = mybir.ActivationFunctionType.Identity
 
 P = 128
 E = 512
-H = 256
+H = E // 2
 GROUPS = 8
 SLABS = 4
-Q_, K_, V_ = 0, 1, 2
+Q, K, V = 0, 1, 2
 
-FLOPS = 2 * 4096 * 512 * 512 * 4
-
-K_ON_V = ((7, 3), (7, 2))
-LOAD_ORDER = ('xa', 'pa', 1, 'xb', 'pb', 0, 2)
-PLAN0 = (
-    ("lx", 0, 1), ("tWe", 0, 0), ("tbe", 0, 0), ("tWe", 1, 0), ("xt", 0, 0), ("tposh", 0, 0),
-    ("tW", 2, 0), ("QWe", 0, 0), ("tW", 3, 0), ("Qx", 0, 0), ("s1", 0, 0), ("pos", 1, 0),
-    ("bb", 1, 0), ("pos", 0, 0), ("s1", 1, 0), ("xt", 1, 0), ("e1", 0, 0), ("QW", 1, 0),
-    ("lx", 0, 2), ("tW", 0, 0), ("e1", 1, 0), ("tposh", 1, 0), ("Qxe", 0, 0), ("tW", 1, 0),
-    ("Qx", 1, 0), ("k", 0, 0), ("k", 1, 0), ("xk", 0, 0), ("pos", 2, 0), ("xk", 1, 0),
-    ("QW", 0, 0), ("stk", 0, 0), ("bb", 0, 0), ("pos", 3, 0), ("s1", 3, 0), ("s1", 2, 0),
-    ("bb", 2, 0), ("e1", 2, 0), ("tW", 4, 0), ("q", 1, 0), ("e1", 3, 0), ("xq", 1, 0),
-    ("q", 0, 0), ("tW", 5, 0), ("Qxe", 1, 0), ("bvp", 0, 0), ("xt", 0, 1), ("xq", 0, 0),
-    ("k", 2, 0), ("QW", 2, 0), ("q", 2, 0), ("k", 3, 0), ("xq", 2, 0), ("xk", 2, 0),
-    ("v", 0, 0), ("q", 3, 0), ("lx", 0, 3), ("xq", 3, 0), ("lx", 0, 4), ("xt", 1, 1),
-    ("v", 1, 0), ("xv", 0, 0), ("cm", 0, 0), ("xk", 3, 0), ("xt", 0, 2), ("xt", 1, 2),
-    ("cb", 0, 0), ("v", 2, 0), ("v", 3, 0), ("cm", 1, 0), ("Qx", 2, 1), ("cb", 1, 0),
-    ("s1", 0, 1), ("e1", 0, 1), ("s1", 2, 1), ("e1", 2, 1), ("s1", 1, 1), ("s1", 3, 1),
-    ("Qx", 2, 2), ("stk", 1, 0), ("stq", 0, 0), ("ct", 0, 0), ("e1", 1, 1), ("stv", 0, 0),
-    ("e1", 3, 1), ("s1", 0, 2), ("stq", 1, 0), ("xv", 1, 0), ("ct", 1, 0), ("s1", 1, 2),
-    ("stv", 1, 0), ("Qxe", 2, 1), ("e1", 0, 2), ("e1", 1, 2),
-)
-PLAN = (
-    ("k", 0, 0), ("q", 0, 0), ("cm", 0, 0), ("xq", 0, 0), ("lx", 0, 4), ("s1", 2, 1),
-    ("v", 0, 0), ("xk", 0, 0), ("cm", 1, 0), ("cb", 0, 0), ("s1", 3, 1), ("k", 1, 0),
-    ("cb", 1, 0), ("xk", 1, 0), ("e1", 2, 1), ("q", 1, 0), ("v", 1, 0), ("e1", 3, 1),
-    ("xq", 1, 0), ("xt", 0, 2), ("stq", 0, 0), ("xt", 1, 2), ("q", 2, 0), ("k", 2, 0),
-    ("xv", 0, 0), ("stk", 0, 0), ("ct", 0, 0), ("k", 3, 0), ("q", 3, 0), ("xk", 3, 0),
-    ("v", 2, 0), ("stv", 0, 0), ("xq", 2, 0), ("v", 3, 0), ("xk", 2, 0), ("Qxe", 2, 1),
-    ("Qx", 2, 2), ("xq", 3, 0), ("ct", 1, 0), ("stq", 1, 0), ("s1", 0, 2), ("xv", 1, 0),
-    ("s1", 1, 2), ("e1", 0, 2), ("stv", 1, 0), ("e1", 1, 2), ("stk", 1, 0),
-)
-PLAN_LAST = (
-    ("cm", 0, 0), ("cb", 0, 0), ("k", 0, 0), ("cm", 1, 0), ("cb", 1, 0), ("xk", 0, 0),
-    ("v", 0, 0), ("k", 1, 0), ("ct", 0, 0), ("ct", 1, 0), ("q", 1, 0), ("v", 1, 0),
-    ("svh", 1, 0), ("xk", 1, 0), ("xq", 1, 0), ("q", 0, 0), ("q", 3, 0), ("xq", 0, 0),
-    ("v", 2, 0), ("xv", 0, 0), ("xq", 3, 0), ("stq", 0, 0), ("v", 3, 0), ("xv", 1, 0),
-    ("k", 3, 0), ("k", 2, 0), ("q", 2, 0), ("xq", 2, 0), ("stk", 0, 0), ("xk", 3, 0),
-    ("sq", 3, 0), ("sq", 2, 0), ("xk", 2, 0), ("sk", 3, 0), ("svl", 1, 0), ("sk", 2, 0),
-    ("stv", 0, 0),
-)
+FLOPS = 2 * GROUPS * SLABS * P * E * E * 4
 
 
 def tile_attention_pa_t_kernel(
@@ -74,10 +34,10 @@ def tile_attention_pa_t_kernel(
         raws = ctx.enter_context(tc.tile_pool(name="raws", bufs=1))
         work = ctx.enter_context(tc.tile_pool(name="work", bufs=2))
         stage = ctx.enter_context(tc.tile_pool(name="stage", bufs=4))
-        tp_pool = ctx.enter_context(tc.psum_pool(name="tp", bufs=2))
+        turn_pool = ctx.enter_context(tc.psum_pool(name="turn", bufs=2))
         s1_pool = ctx.enter_context(tc.psum_pool(name="s1", bufs=2))
         s2_pool = ctx.enter_context(tc.psum_pool(name="s2", bufs=3))
-        vb_pool = ctx.enter_context(tc.psum_pool(name="vb", bufs=1))
+        vlow_pool = ctx.enter_context(tc.psum_pool(name="vlow", bufs=1))
         ctx.enter_context(tc.manual_schedule())
 
         def bank_of(pool, tag):
@@ -89,71 +49,69 @@ def tile_attention_pa_t_kernel(
         nc.vector.memset(be_rows[:].bitcast(I32), 0)
         ones = consts.tile([P, P], BF16)
         nc.vector.memset(ones[:], 1.0)
-        rows = consts.tile([P, 3 * E], BF16)
-        nc.vector.memset(rows[:].bitcast(I32), 0)
+        bias_rows = consts.tile([P, 3 * E], BF16)
+        nc.vector.memset(bias_rows[:].bitcast(I32), 0)
 
         nc.sync.dma_start(out=be_rows[0:2, :], in_=b_embed.rearrange("(u w) -> u w", u=2))
         we_raw = raws.tile([P, 4 * E], BF16)
         we_view = W_embed.rearrange("(u m e) k -> u m (e k)", u=2, e=2)
-        for u in range(2):
-            nc.sync.dma_start(out=we_raw[:, 2 * E * u : 2 * E * (u + 1)], in_=we_view[u])
-        x_raw = []
-        for g in range(GROUPS):
-            x_raw.append(raws.tile([P, 4 * E], BF16, name="x_raw%d" % g))
-        x0_view = x[0].rearrange("(c j) a d -> c (j a d)", j=SLABS)
+        x_raw = [raws.tile([P, 4 * E], BF16, name="x_raw%d" % g) for g in range(GROUPS)]
+        x_views = [x[g].rearrange("(c j) a d -> c (j a d)", j=SLABS) for g in range(GROUPS)]
         pos_raw = raws.tile([P, 4 * E], BF16)
         pos_view = pos_embed.rearrange("(c j) e -> c (j e)", j=SLABS)
-        w_raw = []
-        for o in range(3):
-            w_raw.append(raws.tile([P, 4 * E], BF16, name="w_raw%d" % o))
-
-        def load_half(dst, view, h):
+        w_raw = [raws.tile([P, 4 * E], BF16, name="w_raw%d" % o) for o in range(3)]
+        for half in range(2):
+            nc.sync.dma_start(out=we_raw[:, 2 * E * half : 2 * E * (half + 1)], in_=we_view[half])
+        for dst, view in ((x_raw[0], x_views[0]), (pos_raw, pos_view)):
+            for half in range(2):
+                cols = slice(2 * E * half, 2 * E * (half + 1))
+                nc.sync.dma_start(out=dst[:, cols], in_=view[:, cols])
+        for o in (K, Q, V):
             nc.sync.dma_start(
-                out=dst[:, 2 * E * h : 2 * E * (h + 1)], in_=view[:, 2 * E * h : 2 * E * (h + 1)]
+                out=w_raw[o][:], in_=weights[o].rearrange("(m s) k -> m (s k)", s=SLABS)
             )
+            nc.sync.dma_start(
+                out=bias_rows[0:1, E * o : E * (o + 1)],
+                in_=biases[o].rearrange("(o n) -> o n", o=1),
+            )
+        for g in range(1, GROUPS):
+            nc.sync.dma_start(out=x_raw[g][:], in_=x_views[g])
 
-        for what in LOAD_ORDER:
-            if what == "xa":
-                load_half(x_raw[0], x0_view, 0)
-            elif what == "xb":
-                load_half(x_raw[0], x0_view, 1)
-            elif what == "pa":
-                load_half(pos_raw, pos_view, 0)
-            elif what == "pb":
-                load_half(pos_raw, pos_view, 1)
-            else:
-                nc.sync.dma_start(
-                    out=w_raw[what][:], in_=weights[what].rearrange("(m s) k -> m (s k)", s=SLABS)
-                )
-                nc.sync.dma_start(
-                    out=rows[0:1, E * what : E * (what + 1)],
-                    in_=biases[what].rearrange("(o n) -> o n", o=1),
-                )
+        we_mx = (
+            consts.tile([P, E], U32, align_bytes=64, name="we_codes"),
+            consts.tile([P, E], U8, align_bytes=64, name="we_scales"),
+        )
+        w_mx = [
+            (
+                consts.tile([P, E], U32, align_bytes=64, name="w_codes%d" % o),
+                consts.tile([P, E], U8, align_bytes=64, name="w_scales%d" % o),
+            )
+            for o in range(3)
+        ]
+        bias_all = consts.tile([P, 3 * E], F32)
+        be_col = consts.tile([P, 4], F32)
+        bv_col = consts.tile([P, 2], F32)
+        pos_t = consts.tile([P, 4 * E], F32)
 
-        we_codes = consts.tile([P, E], U32, align_bytes=64)
-        we_scales = consts.tile([P, E], U8, align_bytes=64)
-        w_codes = []
-        w_scales = []
-        for o in range(3):
-            w_codes.append(consts.tile([P, E], U32, align_bytes=64, name="w_codes%d" % o))
-            w_scales.append(consts.tile([P, E], U8, align_bytes=64, name="w_scales%d" % o))
-        bias_bc = consts.tile([P, 3 * E], F32)
-        be_pp = consts.tile([P, 4], F32)
-        bv_pp = consts.tile([P, 2], F32)
-        posbT = consts.tile([P, 4 * E], F32)
-
-        live = {}
-        done = set()
-
-        def need(*keys):
-            for key in keys:
-                assert key in done, key
+        grouped_x = {}
+        x_mx = {}
+        grouped_xe = {}
+        xe_mx = {}
+        banks = {}
+        staged = {}
+        v_high = {}
 
         def new_grouped():
             grouped = work.tile([P, 4 * E], BF16, align_bytes=64, tag="grouped", bufs=4)
             return grouped
 
-        def flip_half(raw, grouped, half, interleaved, pool, tag, engine):
+        def new_mx(tag):
+            return (
+                work.tile([P, E], U32, align_bytes=64, tag=tag + "_codes", name=tag + "_codes"),
+                work.tile([P, E], U8, align_bytes=64, tag=tag + "_scales", name=tag + "_scales"),
+            )
+
+        def turn_words(raw, half, pool, tag):
             words = raw[:].bitcast(F32)
             bank = bank_of(pool, tag)
             for i in range(4):
@@ -162,265 +120,247 @@ def tile_attention_pa_t_kernel(
                     words[:, E * half + P * i : E * half + P * (i + 1)],
                     ident[:],
                 )
+            return bank
+
+        def turn_half(raw, grouped, half, rows_interleaved, copy):
+            bank = turn_words(raw, half, turn_pool, "turn")
             gwords = grouped[:].bitcast(F32)
-            if interleaved:
-                dst = gwords.rearrange("p (m s u) -> p m s u", s=4, u=2)[
-                    :, :, 2 * half : 2 * half + 2, :
-                ]
-                src = bank[:].rearrange("p (s u m) -> p m s u", s=2, u=2)
+            if rows_interleaved:
+                copy(
+                    out=gwords.rearrange("p (m s u) -> p m s u", s=4, u=2)[
+                        :, :, 2 * half : 2 * half + 2, :
+                    ],
+                    in_=bank[:].rearrange("p (s u m) -> p m s u", s=2, u=2),
+                )
             else:
-                dst = gwords.rearrange("p (s m u) -> p s m u", s=4, u=2)[
-                    :, 2 * half : 2 * half + 2, :, :
-                ]
-                src = bank[:].rearrange("p (s u m) -> p s m u", s=2, u=2)
-            if engine == "V":
-                nc.vector.tensor_copy(out=dst, in_=src)
-            else:
-                nc.scalar.copy(out=dst, in_=src)
+                copy(
+                    out=gwords.rearrange("p (s m u) -> p s m u", s=4, u=2)[
+                        :, 2 * half : 2 * half + 2, :, :
+                    ],
+                    in_=bank[:].rearrange("p (s u m) -> p s m u", s=2, u=2),
+                )
 
-        def quantise(grouped, codes, scales, c0, c1):
-            nc.vector.quantize_mx(
-                out=codes[:, c0:c1].bitcast(FP8X4),
-                scales=scales[:, c0:c1],
-                in_=grouped[:, 4 * c0 : 4 * c1],
-            )
+        def turn_x(g):
+            grouped_x[g] = new_grouped()
+            for half in range(2):
+                turn_half(x_raw[g], grouped_x[g], half, False, nc.scalar.copy)
 
-        def mx_pair(tag):
-            codes = work.tile([P, E], U32, align_bytes=64, tag=tag + "_codes", name=tag + "_codes")
-            scales = work.tile([P, E], U8, align_bytes=64, tag=tag + "_scales", name=tag + "_scales")
-            return (codes, scales)
+        def quantise(grouped, mx):
+            nc.vector.quantize_mx(out=mx[0][:].bitcast(FP8X4), scales=mx[1][:], in_=grouped[:])
 
-        def st_tile(g, o, pair):
-            key = ("st", g, o, pair)
-            if key not in live:
-                live[key] = stage.tile([P, 2 * E], F32, name="st%d" % o, tag="st%d" % o)
-            return live[key]
+        def quantise_x(g):
+            x_mx[g] = new_mx("x")
+            quantise(grouped_x[g], x_mx[g])
 
-        def mx(out, lhsT, l0, l1, rhs, r0, r1):
+        def quantise_xe(g):
+            xe_mx[g] = new_mx("xe")
+            quantise(grouped_xe[g], xe_mx[g])
+
+        def mx_pass(out, stationary, s_cols, moving, m_cols):
             nc.tensor.matmul_mx(
                 out=out,
-                lhsT=lhsT[0][:, l0:l1].bitcast(FP8X4),
-                lhsT_scale=lhsT[1][:, l0:l1],
-                rhs=rhs[0][:, r0:r1].bitcast(FP8X4),
-                rhs_scale=rhs[1][:, r0:r1],
+                lhsT=stationary[0][:, s_cols].bitcast(FP8X4),
+                lhsT_scale=stationary[1][:, s_cols],
+                rhs=moving[0][:, m_cols].bitcast(FP8X4),
+                rhs_scale=moving[1][:, m_cols],
                 start=True,
                 stop=True,
             )
 
-        def do(op, a, g):
-            if g >= GROUPS:
-                return
-            key = (op, a, g)
-            assert key not in done, key
-            pair = a // 2
-            if op == "lx":
-                nc.sync.dma_start(
-                    out=x_raw[g][:], in_=x[g].rearrange("(c j) a d -> c (j a d)", j=SLABS)
-                )
-            elif op == "tWe":
-                if a == 0:
-                    live["gwe"] = new_grouped()
-                flip_half(we_raw, live["gwe"], a, False, tp_pool, "tp", "VS"[a])
-            elif op == "QWe":
-                need(("tWe", 0, 0), ("tWe", 1, 0))
-                quantise(live["gwe"], we_codes, we_scales, 0, E)
-            elif op == "tbe":
-                bank = bank_of(s2_pool, "s2")
-                nc.tensor.transpose(bank[:, 0:P], be_rows[:].bitcast(F32), ident[:])
-                nc.scalar.copy(out=be_pp[:], in_=bank[:].bitcast(BF16)[:, 0:4])
-            elif op == "tposh":
-                words = pos_raw[:].bitcast(F32)
-                bank = bank_of((s2_pool, vb_pool)[a], ("s2", "vb")[a])
-                for i in range(4):
-                    nc.tensor.transpose(
-                        bank[:, P * i : P * (i + 1)],
-                        words[:, E * a + P * i : E * a + P * (i + 1)],
-                        ident[:],
-                    )
-                live[("posbank", a)] = bank
-            elif op == "pos":
-                need(("tposh", pair, 0), ("tbe", 0, 0))
-                nc.vector.tensor_tensor(
-                    out=posbT[:, E * a : E * (a + 1)].rearrange("p (c u e) -> p c u e", u=2, e=2),
-                    in0=live[("posbank", pair)][:]
-                    .bitcast(BF16)
-                    .rearrange("p (s u c e) -> p s c u e", s=2, u=2, e=2)[:, a % 2],
-                    in1=be_pp[:]
-                    .rearrange("p (o u e) -> p o u e", o=1, u=2)
-                    .to_broadcast([P, P, 2, 2]),
-                    op=ADD,
-                )
-            elif op == "tW":
-                if a % 2 == 0:
-                    live[("gw", pair)] = new_grouped()
-                else:
-                    need(("tW", a - 1, 0))
-                flip_half(w_raw[pair], live[("gw", pair)], a % 2, True, tp_pool, "tp", "S")
-            elif op == "QW":
-                need(("tW", 2 * a, 0), ("tW", 2 * a + 1, 0))
-                quantise(live[("gw", a)], w_codes[a], w_scales[a], 0, E)
-            elif op == "bb":
-                bank = bank_of(s2_pool, "s2")
-                nc.tensor.matmul(
-                    out=bank[:], lhsT=ones[:], rhs=rows[:, E * a : E * (a + 1)], start=True, stop=True
-                )
-                nc.scalar.copy(out=bias_bc[:, E * a : E * (a + 1)], in_=bank[:])
-            elif op == "bvp":
-                need(("bb", V_, 0))
-                bank = bank_of(s2_pool, "s2")
+        def block(i):
+            return slice(P * i, P * (i + 1))
+
+        def stage1_passes(g, j, pool, tag):
+            bank = bank_of(pool, tag)
+            for t in range(4):
+                mx_pass(bank[:, block(t)], we_mx, block(t), x_mx[g], block(j))
+            banks[("s1", j)] = bank
+
+        def stage1_exit(g, j):
+            if j == 0:
+                grouped_xe[g] = work.tile([P, 4 * E], BF16, align_bytes=64, tag="xe", name="xe")
+            cols = slice(E * j, E * (j + 1))
+            nc.vector.tensor_tensor(
+                out=grouped_xe[g][:, cols].rearrange("p (c t) -> p c t", t=4),
+                in0=banks[("s1", j)][:].rearrange("p (t c) -> p c t", t=4),
+                in1=pos_t[:, cols].rearrange("p (c t) -> p c t", t=4),
+                op=ADD,
+            )
+
+        def staged_slab(o, j):
+            if j % 2 == 0:
+                staged[(o, j // 2)] = stage.tile([P, 2 * E], F32, name="st%d" % o, tag="st%d" % o)
+            return staged[(o, j // 2)][:, E * (j % 2) : E * (j % 2 + 1)]
+
+        def full_pass(g, j, o):
+            banks[o] = bank_of(s2_pool, "s2")
+            mx_pass(banks[o][:], xe_mx[g], block(j), w_mx[o], slice(0, E))
+
+        def q_exit(j):
+            nc.vector.tensor_tensor(
+                out=staged_slab(Q, j), in0=banks[Q][:], in1=bias_all[:, E * Q : E * (Q + 1)], op=ADD
+            )
+
+        def k_exit(j):
+            slab = staged_slab(K, j)
+            nc.scalar.copy(out=slab, in_=banks[K][:])
+            nc.gpsimd.tensor_tensor(
+                out=slab, in0=slab, in1=bias_all[:, E * K : E * (K + 1)], op=ADD
+            )
+
+        def v_low_pass(g, j):
+            if j % 2 == 0:
+                banks[V] = bank_of(vlow_pool, "vlow")
+                staged[(V, j // 2)] = stage.tile([P, 2 * E], F32, name="st2", tag="st2")
+            mx_pass(
+                banks[V][:, H * (j % 2) : H * (j % 2 + 1)], xe_mx[g], block(j), w_mx[V], slice(0, H)
+            )
+
+        def v_low_exit(pair):
+            nc.vector.tensor_tensor(
+                out=staged[(V, pair)][:].rearrange("c (j e) -> c j e", j=2)[:, :, 0:H],
+                in0=banks[V][:].rearrange("c (j e) -> c j e", j=2),
+                in1=bias_all[:, E * V : E * V + H].unsqueeze(1).to_broadcast([P, 2, H]),
+                op=ADD,
+            )
+
+        def v_high_pass(g, i):
+            banks[("vh", i)] = bank_of(s2_pool, "s2")
+            mx_pass(banks[("vh", i)][:], w_mx[V], slice(H + P * i, H + P * (i + 1)), xe_mx[g], slice(0, E))
+
+        def v_high_bias(i):
+            v_high[i] = work.tile([P, E], F32, tag="v_high", name="v_high", bufs=4)
+            nc.scalar.activation(
+                out=v_high[i][:], in_=banks[("vh", i)][:], func=IDENTITY, bias=bv_col[:, i : i + 1]
+            )
+
+        def v_high_back(pair):
+            bank = bank_of(turn_pool, "turn")
+            for j2 in range(2):
                 for i in range(2):
                     nc.tensor.transpose(
-                        bank[:, P * i : P * (i + 1)],
-                        bias_bc[:, E * V_ + H + P * i : E * V_ + H + P * (i + 1)],
-                        ident[:],
+                        bank[:, block(2 * j2 + i)], v_high[i][:, block(2 * pair + j2)], ident[:]
                     )
-                nc.scalar.copy(
-                    out=bv_pp[:].unsqueeze(2),
-                    in_=bank[:].rearrange("p (i c) -> p i c", c=P)[:, 0:2, 0:1],
-                )
-            elif op == "xt":
-                if g > 0:
-                    need(("lx", 0, g))
-                if a == 0:
-                    live[("gx", g)] = new_grouped()
-                else:
-                    need(("xt", 0, g))
-                flip_half(x_raw[g], live[("gx", g)], a, False, tp_pool, "tp", "S")
-            elif op == "Qx":
-                if a in (0, 2):
-                    live[("x", g)] = mx_pair("x")
-                if a == 1:
-                    need(("Qx", 0, g))
-                need(*[("xt", h, g) for h in ((0, 1) if a == 2 else (a,))])
-                c0, c1 = ((0, H), (H, E), (0, E))[a]
-                quantise(live[("gx", g)], live[("x", g)][0], live[("x", g)][1], c0, c1)
-                if a == 2:
-                    done.add(("Qx", 0, g))
-                    done.add(("Qx", 1, g))
-            elif op == "s1":
-                need(("Qx", pair, g), ("QWe", 0, 0))
-                bank = bank_of(s1_pool, "s1")
-                for t in range(4):
-                    mx(bank[:, P * t : P * (t + 1)], (we_codes, we_scales), P * t, P * (t + 1),
-                       live[("x", g)], P * a, P * (a + 1))
-                live[("s1", g, a)] = bank
-            elif op == "e1":
-                need(("s1", a, g), ("pos", a, 0))
-                if ("gxe", g) not in live:
-                    gxe = work.tile([P, 4 * E], BF16, align_bytes=64, tag="gxe")
-                    live[("gxe", g)] = gxe
-                nc.vector.tensor_tensor(
-                    out=live[("gxe", g)][:, E * a : E * (a + 1)].rearrange("p (c t) -> p c t", t=4),
-                    in0=live[("s1", g, a)][:].rearrange("p (t c) -> p c t", t=4),
-                    in1=posbT[:, E * a : E * (a + 1)].rearrange("p (c t) -> p c t", t=4),
-                    op=ADD,
-                )
-            elif op == "Qxe":
-                if a in (0, 2):
-                    live[("xe", g)] = mx_pair("xe")
-                if a == 1:
-                    need(("Qxe", 0, g))
-                need(*[("e1", j, g) for j in ((0, 1), (2, 3), (0, 1, 2, 3))[a]])
-                c0, c1 = ((0, H), (H, E), (0, E))[a]
-                quantise(live[("gxe", g)], live[("xe", g)][0], live[("xe", g)][1], c0, c1)
-                if a == 2:
-                    done.add(("Qxe", 0, g))
-                    done.add(("Qxe", 1, g))
-            elif op in ("k", "q"):
-                o = K_ if op == "k" else Q_
-                need(("Qxe", pair, g), ("QW", o, 0))
-                bank = bank_of(s2_pool, "s2")
-                mx(bank[:], live[("xe", g)], P * a, P * (a + 1), (w_codes[o], w_scales[o]), 0, E)
-                live[(op, g, a)] = bank
-            elif op in ("xk", "xq"):
-                o = K_ if op == "xk" else Q_
-                need((op[1], a, g), ("bb", o, 0))
-                dst = st_tile(g, o, pair)[:, E * (a % 2) : E * (a % 2 + 1)]
-                bias = bias_bc[:, E * o : E * (o + 1)]
-                bank = live[(op[1], g, a)]
-                if o == K_ and (g, a) not in K_ON_V:
-                    nc.scalar.copy(out=dst, in_=bank[:])
-                    nc.gpsimd.tensor_tensor(out=dst, in0=dst, in1=bias, op=ADD)
-                else:
-                    nc.vector.tensor_tensor(out=dst, in0=bank[:], in1=bias, op=ADD)
-            elif op == "v":
-                need(("Qxe", pair, g), ("QW", V_, 0))
-                if a % 2 == 0:
-                    live[("v", g, pair)] = bank_of(vb_pool, "vb")
-                else:
-                    need(("v", a - 1, g))
-                mx(live[("v", g, pair)][:, H * (a % 2) : H * (a % 2 + 1)], live[("xe", g)],
-                   P * a, P * (a + 1), (w_codes[V_], w_scales[V_]), 0, H)
-            elif op == "xv":
-                need(("v", 2 * a, g), ("v", 2 * a + 1, g), ("bb", V_, 0))
-                nc.vector.tensor_tensor(
-                    out=st_tile(g, V_, a)[:].rearrange("c (j e) -> c j e", j=2)[:, :, 0:H],
-                    in0=live[("v", g, a)][:].rearrange("c (j e) -> c j e", j=2),
-                    in1=bias_bc[:, E * V_ : E * V_ + H].unsqueeze(1).to_broadcast([P, 2, H]),
-                    op=ADD,
-                )
-            elif op == "cm":
-                need(("Qxe", 0, g), ("Qxe", 1, g), ("QW", V_, 0))
-                bank = bank_of(s2_pool, "s2")
-                mx(bank[:], (w_codes[V_], w_scales[V_]), H + P * a, H + P * (a + 1), live[("xe", g)], 0, E)
-                live[("cm", g, a)] = bank
-            elif op == "cb":
-                need(("cm", a, g), ("bvp", 0, 0))
-                tmp = work.tile([P, E], F32, tag="c_tmp", bufs=4)
-                nc.scalar.activation(
-                    out=tmp[:], in_=live[("cm", g, a)][:], func=IDENTITY, bias=bv_pp[:, a : a + 1]
-                )
-                live[("cb", g, a)] = tmp
-            elif op == "ct":
-                need(("cb", 0, g), ("cb", 1, g))
-                bank = bank_of(tp_pool, "tp")
-                for j2 in range(2):
-                    for i in range(2):
-                        nc.tensor.transpose(
-                            bank[:, P * (2 * j2 + i) : P * (2 * j2 + i + 1)],
-                            live[("cb", g, i)][:, P * (2 * a + j2) : P * (2 * a + j2 + 1)],
-                            ident[:],
-                        )
-                nc.scalar.copy(
-                    out=st_tile(g, V_, a)[:].rearrange("c (j e) -> c j e", j=2)[:, :, H:E],
-                    in_=bank[:].rearrange("c (j e) -> c j e", j=2),
-                )
-            elif op in ("stq", "stk", "stv"):
-                o = {"stq": Q_, "stk": K_, "stv": V_}[op]
-                if o == V_:
-                    need(("xv", a, g), ("ct", a, g))
-                else:
-                    need(("x" + op[2], 2 * a, g), ("x" + op[2], 2 * a + 1, g))
-                nc.sync.dma_start(
-                    out=outs[o][g].rearrange("(c j) h d -> c (j h d)", j=SLABS)[
-                        :, 2 * E * a : 2 * E * (a + 1)
-                    ],
-                    in_=live[("st", g, o, a)][:],
-                )
-            elif op in ("sq", "sk"):
-                o = {"sq": Q_, "sk": K_}[op]
-                need(("x" + op[1], a, g))
-                nc.sync.dma_start(
-                    out=outs[o][g].rearrange("(c j) h d -> c (j h d)", j=SLABS)[:, E * a : E * (a + 1)],
-                    in_=live[("st", g, o, pair)][:, E * (a % 2) : E * (a % 2 + 1)],
-                )
-            elif op in ("svl", "svh"):
-                need(("xv", a, g) if op == "svl" else ("ct", a, g))
-                e0 = 0 if op == "svl" else H
-                nc.sync.dma_start(
-                    out=outs[V_][g].rearrange("(c j) h d -> c j (h d)", j=SLABS)[
-                        :, 2 * a : 2 * a + 2, e0 : e0 + H
-                    ],
-                    in_=live[("st", g, V_, a)][:].rearrange("c (j e) -> c j e", j=2)[:, :, e0 : e0 + H],
-                )
-            else:
-                assert False, op
-            done.add(key)
+            nc.scalar.copy(
+                out=staged[(V, pair)][:].rearrange("c (j e) -> c j e", j=2)[:, :, H:E],
+                in_=bank[:].rearrange("c (j e) -> c j e", j=2),
+            )
 
-        for op, a, dg in PLAN0:
-            do(op, a, dg)
-        for g in range(1, GROUPS - 1):
-            for op, a, dg in PLAN:
-                do(op, a, g + dg)
-        for op, a, dg in PLAN_LAST:
-            do(op, a, GROUPS - 1 + dg)
+        def store(g, o, pair):
+            nc.sync.dma_start(
+                out=outs[o][g].rearrange("(c j) h d -> c (j h d)", j=SLABS)[
+                    :, 2 * E * pair : 2 * E * (pair + 1)
+                ],
+                in_=staged[(o, pair)][:],
+            )
+
+        grouped_we = new_grouped()
+        turn_half(we_raw, grouped_we, 0, False, nc.vector.tensor_copy)
+        turn_half(we_raw, grouped_we, 1, False, nc.scalar.copy)
+        turn_x(0)
+        be_bank = bank_of(s2_pool, "s2")
+        nc.tensor.transpose(be_bank[:, 0:P], be_rows[:].bitcast(F32), ident[:])
+        nc.scalar.copy(out=be_col[:], in_=be_bank[:].bitcast(BF16)[:, 0:4])
+        pos_banks = [turn_words(pos_raw, 0, s2_pool, "s2"), turn_words(pos_raw, 1, vlow_pool, "vlow")]
+        quantise(grouped_we, we_mx)
+        quantise_x(0)
+        grouped_w = {}
+
+        def turn_weight(o):
+            grouped_w[o] = new_grouped()
+            for half in range(2):
+                turn_half(w_raw[o], grouped_w[o], half, True, nc.scalar.copy)
+
+        def spread_bias(o):
+            bank = bank_of(s2_pool, "s2")
+            cols = slice(E * o, E * (o + 1))
+            nc.tensor.matmul(out=bank[:], lhsT=ones[:], rhs=bias_rows[:, cols], start=True, stop=True)
+            nc.scalar.copy(out=bias_all[:, cols], in_=bank[:])
+
+        turn_weight(K)
+        for j in range(SLABS):
+            if j < 2:
+                stage1_passes(0, j, s1_pool, "s1")
+            else:
+                stage1_passes(0, j, s2_pool, "s2")
+        for j in range(SLABS):
+            nc.vector.tensor_tensor(
+                out=pos_t[:, E * j : E * (j + 1)].rearrange("p (c u e) -> p c u e", u=2, e=2),
+                in0=pos_banks[j // 2][:]
+                .bitcast(BF16)
+                .rearrange("p (s u c e) -> p s c u e", s=2, u=2, e=2)[:, j % 2],
+                in1=be_col[:].rearrange("p (o u e) -> p o u e", o=1, u=2).to_broadcast([P, P, 2, 2]),
+                op=ADD,
+            )
+        for j in range(SLABS):
+            stage1_exit(0, j)
+        spread_bias(K)
+        turn_weight(Q)
+        spread_bias(Q)
+        turn_x(1)
+        turn_weight(V)
+        spread_bias(V)
+        bv_bank = bank_of(s2_pool, "s2")
+        for i in range(2):
+            nc.tensor.transpose(
+                bv_bank[:, block(i)], bias_all[:, E * V + H + P * i : E * V + H + P * (i + 1)], ident[:]
+            )
+        nc.scalar.copy(
+            out=bv_col[:].unsqueeze(2),
+            in_=bv_bank[:].rearrange("p (i c) -> p i c", c=P)[:, 0:2, 0:1],
+        )
+        quantise(grouped_w[K], w_mx[K])
+        quantise(grouped_w[Q], w_mx[Q])
+        quantise_xe(0)
+        quantise_x(1)
+        quantise(grouped_w[V], w_mx[V])
+        for j in range(2):
+            stage1_passes(1, j, s1_pool, "s1")
+        for j in range(2):
+            stage1_exit(1, j)
+
+        for g in range(GROUPS):
+            for j in range(SLABS):
+                full_pass(g, j, K)
+                full_pass(g, j, Q)
+                v_low_pass(g, j)
+                if j == 0:
+                    v_high_pass(g, 0)
+                    v_high_pass(g, 1)
+                k_exit(j)
+                if j < 3:
+                    q_exit(j)
+                if j == 0:
+                    v_high_bias(0)
+                    v_high_bias(1)
+                    if g + 1 < GROUPS:
+                        stage1_passes(g + 1, 2, s1_pool, "s1")
+                        stage1_passes(g + 1, 3, s1_pool, "s1")
+                        stage1_exit(g + 1, 2)
+                        stage1_exit(g + 1, 3)
+                if j == 1:
+                    v_low_exit(0)
+                    if g + 2 < GROUPS:
+                        turn_x(g + 2)
+                    store(g, Q, 0)
+                if j == 2:
+                    v_high_back(0)
+                    v_high_back(1)
+                if j == 3:
+                    store(g, K, 0)
+                    store(g, V, 0)
+                    if g + 2 < GROUPS:
+                        quantise_x(g + 2)
+                    if g + 1 < GROUPS:
+                        quantise_xe(g + 1)
+                    if g + 2 < GROUPS:
+                        stage1_passes(g + 2, 0, s1_pool, "s1")
+                        stage1_passes(g + 2, 1, s1_pool, "s1")
+                    q_exit(j)
+                    v_low_exit(1)
+                    if g + 2 < GROUPS:
+                        stage1_exit(g + 2, 0)
+                        stage1_exit(g + 2, 1)
+                    store(g, Q, 1)
+                    store(g, V, 1)
+                    store(g, K, 1)

@@ -51,8 +51,9 @@ def tile_attention_pa_t_kernel(
         nc.vector.memset(ones[:], 1.0)
         bias_rows = consts.tile([P, 3 * E], BF16)
         nc.vector.memset(bias_rows[:].bitcast(I32), 0)
+        warm = consts.tile([P, 1], F32)
+        nc.scalar.activation(out=warm[:], in_=ones[:, 0:1], func=IDENTITY)
 
-        nc.sync.dma_start(out=be_rows[0:2, :], in_=b_embed.rearrange("(u w) -> u w", u=2))
         we_raw = raws.tile([P, 4 * E], BF16)
         we_view = W_embed.rearrange("(u m e) k -> u m (e k)", u=2, e=2)
         x_raw = [raws.tile([P, 4 * E], BF16, name="x_raw%d" % g) for g in range(GROUPS)]
@@ -62,6 +63,7 @@ def tile_attention_pa_t_kernel(
         w_raw = [raws.tile([P, 4 * E], BF16, name="w_raw%d" % o) for o in range(3)]
         for half in range(2):
             nc.sync.dma_start(out=we_raw[:, 2 * E * half : 2 * E * (half + 1)], in_=we_view[half])
+        nc.sync.dma_start(out=be_rows[0:2, :], in_=b_embed.rearrange("(u w) -> u w", u=2))
         for dst, view in ((x_raw[0], x_views[0]), (pos_raw, pos_view)):
             for half in range(2):
                 cols = slice(2 * E * half, 2 * E * (half + 1))
@@ -294,12 +296,18 @@ def tile_attention_pa_t_kernel(
             )
         for j in range(SLABS):
             stage1_exit(0, j)
-        spread_bias(K)
         turn_weight(Q)
-        spread_bias(Q)
         turn_x(1)
         turn_weight(V)
-        spread_bias(V)
+        for o in (V, Q, K):
+            spread_bias(o)
+        quantise(grouped_w[K], w_mx[K])
+        quantise(grouped_w[Q], w_mx[Q])
+        quantise_xe(0)
+        quantise_x(1)
+        quantise(grouped_w[V], w_mx[V])
+        for j in range(2):
+            stage1_passes(1, j, s1_pool, "s1")
         bv_bank = bank_of(s2_pool, "s2")
         for i in range(2):
             nc.tensor.transpose(
@@ -309,13 +317,6 @@ def tile_attention_pa_t_kernel(
             out=bv_col[:].unsqueeze(2),
             in_=bv_bank[:].rearrange("p (i c) -> p i c", c=P)[:, 0:2, 0:1],
         )
-        quantise(grouped_w[K], w_mx[K])
-        quantise(grouped_w[Q], w_mx[Q])
-        quantise_xe(0)
-        quantise_x(1)
-        quantise(grouped_w[V], w_mx[V])
-        for j in range(2):
-            stage1_passes(1, j, s1_pool, "s1")
         for j in range(2):
             stage1_exit(1, j)
 

@@ -34,8 +34,7 @@ def tile_attention_pa_t_kernel(
         raws = ctx.enter_context(tc.tile_pool(name="raws", bufs=1))
         work = ctx.enter_context(tc.tile_pool(name="work", bufs=2))
         stage = ctx.enter_context(tc.tile_pool(name="stage", bufs=4))
-        turn_pool = ctx.enter_context(tc.psum_pool(name="turn", bufs=2))
-        s1_pool = ctx.enter_context(tc.psum_pool(name="s1", bufs=2))
+        prep_pool = ctx.enter_context(tc.psum_pool(name="prep", bufs=4))
         s2_pool = ctx.enter_context(tc.psum_pool(name="s2", bufs=3))
         vlow_pool = ctx.enter_context(tc.psum_pool(name="vlow", bufs=1))
         ctx.enter_context(tc.manual_schedule())
@@ -125,7 +124,7 @@ def tile_attention_pa_t_kernel(
             return bank
 
         def turn_half(raw, grouped, half, rows_interleaved, copy):
-            bank = turn_words(raw, half, turn_pool, "turn")
+            bank = turn_words(raw, half, prep_pool, "prep")
             gwords = grouped[:].bitcast(F32)
             if rows_interleaved:
                 copy(
@@ -237,7 +236,7 @@ def tile_attention_pa_t_kernel(
             )
 
         def v_high_back(pair):
-            bank = bank_of(turn_pool, "turn")
+            bank = bank_of(prep_pool, "prep")
             for j2 in range(2):
                 for i in range(2):
                     nc.tensor.transpose(
@@ -282,7 +281,7 @@ def tile_attention_pa_t_kernel(
         turn_weight(K)
         for j in range(SLABS):
             if j < 2:
-                stage1_passes(0, j, s1_pool, "s1")
+                stage1_passes(0, j, prep_pool, "prep")
             else:
                 stage1_passes(0, j, s2_pool, "s2")
         for j in range(SLABS):
@@ -307,7 +306,7 @@ def tile_attention_pa_t_kernel(
         quantise_x(1)
         quantise(grouped_w[V], w_mx[V])
         for j in range(2):
-            stage1_passes(1, j, s1_pool, "s1")
+            stage1_passes(1, j, prep_pool, "prep")
         bv_bank = bank_of(s2_pool, "s2")
         for i in range(2):
             nc.tensor.transpose(
@@ -322,21 +321,26 @@ def tile_attention_pa_t_kernel(
 
         for g in range(GROUPS):
             for j in range(SLABS):
-                full_pass(g, j, K)
-                full_pass(g, j, Q)
+                for o in (K, Q) if j == 0 else (Q, K):
+                    full_pass(g, j, o)
                 v_low_pass(g, j)
                 if j == 0:
                     v_high_pass(g, 0)
                     v_high_pass(g, 1)
-                k_exit(j)
-                if j < 3:
+                if j == 0:
+                    k_exit(j)
                     q_exit(j)
+                elif j < 3:
+                    q_exit(j)
+                    k_exit(j)
+                else:
+                    k_exit(j)
                 if j == 0:
                     v_high_bias(0)
                     v_high_bias(1)
                     if g + 1 < GROUPS:
-                        stage1_passes(g + 1, 2, s1_pool, "s1")
-                        stage1_passes(g + 1, 3, s1_pool, "s1")
+                        stage1_passes(g + 1, 2, prep_pool, "prep")
+                        stage1_passes(g + 1, 3, prep_pool, "prep")
                         stage1_exit(g + 1, 2)
                         stage1_exit(g + 1, 3)
                 if j == 1:
@@ -355,8 +359,8 @@ def tile_attention_pa_t_kernel(
                     if g + 1 < GROUPS:
                         quantise_xe(g + 1)
                     if g + 2 < GROUPS:
-                        stage1_passes(g + 2, 0, s1_pool, "s1")
-                        stage1_passes(g + 2, 1, s1_pool, "s1")
+                        stage1_passes(g + 2, 0, prep_pool, "prep")
+                        stage1_passes(g + 2, 1, prep_pool, "prep")
                     q_exit(j)
                     v_low_exit(1)
                     if g + 2 < GROUPS:

@@ -37,7 +37,6 @@ def tile_attention_pa_t_kernel(
         prep_pool = ctx.enter_context(tc.psum_pool(name="prep", bufs=4))
         s2_pool = ctx.enter_context(tc.psum_pool(name="s2", bufs=3))
         vlow_pool = ctx.enter_context(tc.psum_pool(name="vlow", bufs=1))
-        ctx.enter_context(tc.manual_schedule())
 
         def bank_of(pool, tag):
             return pool.tile([P, E], F32, tag=tag, name="bank_" + tag)

from contextlib import ExitStack

import concourse.mybir as mybir
from concourse.masks import make_identity

F32 = mybir.dt.float32
BF16 = mybir.dt.bfloat16
U32 = mybir.dt.uint32
U8 = mybir.dt.uint8
I32 = mybir.dt.int32
FP8X4 = mybir.dt.float8_e4m3fn_x4
ADD = mybir.AluOpType.add
IDENTITY = mybir.ActivationFunctionType.Identity

P = 128
E = 512
H = E // 2
GROUPS = 8
SLABS = 4
Q, K, V = 0, 1, 2

FLOPS = 2 * GROUPS * SLABS * P * E * E * 4


def tile_attention_pa_t_kernel(
    tc, x, pos_embed, W_embed, b_embed, Wq, bq, Wk, bk, Wv, bv, out_0, out_1, out_2
):
    nc = tc.nc
    outs = [out_0, out_1, out_2]
    weights = [Wq, Wk, Wv]
    biases = [bq, bk, bv]
    with ExitStack() as ctx:
        consts = ctx.enter_context(tc.tile_pool(name="consts", bufs=1))
        raws = ctx.enter_context(tc.tile_pool(name="raws", bufs=1))
        work = ctx.enter_context(tc.tile_pool(name="work", bufs=2))
        stage = ctx.enter_context(tc.tile_pool(name="stage", bufs=4))
        prep_pool = ctx.enter_context(tc.psum_pool(name="prep", bufs=4))
        s2_pool = ctx.enter_context(tc.psum_pool(name="s2", bufs=3))
        vlow_pool = ctx.enter_context(tc.psum_pool(name="vlow", bufs=1))

        def bank_of(pool, tag):
            return pool.tile([P, E], F32, tag=tag, name="bank_" + tag)

        ident = consts.tile([P, P], F32)
        make_identity(nc, ident[:])
        be_rows = consts.tile([P, H], BF16)
        nc.vector.memset(be_rows[:].bitcast(I32), 0)
        ones = consts.tile([P, P], BF16)
        nc.vector.memset(ones[:], 1.0)
        bias_rows = consts.tile([P, 3 * E], BF16)
        nc.vector.memset(bias_rows[:].bitcast(I32), 0)
        warm = consts.tile([P, 1], F32)
        nc.scalar.activation(out=warm[:], in_=ones[:, 0:1], func=IDENTITY)

        we_raw = raws.tile([P, 4 * E], BF16)
        we_view = W_embed.rearrange("(u m e) k -> u m (e k)", u=2, e=2)
        x_raw = [raws.tile([P, 4 * E], BF16, name="x_raw%d" % g) for g in range(GROUPS)]
        x_views = [x[g].rearrange("(c j) a d -> c (j a d)", j=SLABS) for g in range(GROUPS)]
        pos_raw = raws.tile([P, 4 * E], BF16)
        pos_view = pos_embed.rearrange("(c j) e -> c (j e)", j=SLABS)
        w_raw = [raws.tile([P, 4 * E], BF16, name="w_raw%d" % o) for o in range(3)]
        for half in range(2):
            nc.sync.dma_start(out=we_raw[:, 2 * E * half : 2 * E * (half + 1)], in_=we_view[half])
        nc.sync.dma_start(out=be_rows[0:2, :], in_=b_embed.rearrange("(u w) -> u w", u=2))
        for dst, view in ((x_raw[0], x_views[0]), (pos_raw, pos_view)):
            for half in range(2):
                cols = slice(2 * E * half, 2 * E * (half + 1))
                nc.sync.dma_start(out=dst[:, cols], in_=view[:, cols])
        for o in (K, Q, V):
            nc.sync.dma_start(
                out=w_raw[o][:], in_=weights[o].rearrange("(m s) k -> m (s k)", s=SLABS)
            )
            nc.sync.dma_start(
                out=bias_rows[0:1, E * o : E * (o + 1)],
                in_=biases[o].rearrange("(o n) -> o n", o=1),
            )
        for g in range(1, GROUPS):
            nc.sync.dma_start(out=x_raw[g][:], in_=x_views[g])

        we_mx = (
            consts.tile([P, E], U32, align_bytes=64, name="we_codes"),
            consts.tile([P, E], U8, align_bytes=64, name="we_scales"),
        )
        w_mx = [
            (
                consts.tile([P, E], U32, align_bytes=64, name="w_codes%d" % o),
                consts.tile([P, E], U8, align_bytes=64, name="w_scales%d" % o),
            )
            for o in range(3)
        ]
        bias_all = consts.tile([P, 3 * E], F32)
        be_col = consts.tile([P, 4], F32)
        bv_col = consts.tile([P, 2], F32)
        pos_t = consts.tile([P, 4 * E], F32)

        grouped_x = {}
        x_mx = {}
        grouped_xe = {}
        xe_mx = {}
        banks = {}
        staged = {}
        v_high = {}

        def new_grouped():
            grouped = work.tile([P, 4 * E], BF16, align_bytes=64, tag="grouped", bufs=4)
            return grouped

        def new_mx(tag):
            return (
                work.tile([P, E], U32, align_bytes=64, tag=tag + "_codes", name=tag + "_codes"),
                work.tile([P, E], U8, align_bytes=64, tag=tag + "_scales", name=tag + "_scales"),
            )

        def turn_words(raw, half, pool, tag):
            words = raw[:].bitcast(F32)
            bank = bank_of(pool, tag)
            for i in range(4):
                nc.tensor.transpose(
                    bank[:, P * i : P * (i + 1)],
                    words[:, E * half + P * i : E * half + P * (i + 1)],
                    ident[:],
                )
            return bank

        def turn_half(raw, grouped, half, rows_interleaved, copy):
            bank = turn_words(raw, half, prep_pool, "prep")
            gwords = grouped[:].bitcast(F32)
            if rows_interleaved:
                copy(
                    out=gwords.rearrange("p (m s u) -> p m s u", s=4, u=2)[
                        :, :, 2 * half : 2 * half + 2, :
                    ],
                    in_=bank[:].rearrange("p (s u m) -> p m s u", s=2, u=2),
                )
            else:
                copy(
                    out=gwords.rearrange("p (s m u) -> p s m u", s=4, u=2)[
                        :, 2 * half : 2 * half + 2, :, :
                    ],
                    in_=bank[:].rearrange("p (s u m) -> p s m u", s=2, u=2),
                )

        def turn_x(g):
            grouped_x[g] = new_grouped()
            for half in range(2):
                turn_half(x_raw[g], grouped_x[g], half, False, nc.scalar.copy)

        def quantise(grouped, mx):
            nc.vector.quantize_mx(out=mx[0][:].bitcast(FP8X4), scales=mx[1][:], in_=grouped[:])

        def quantise_x(g):
            x_mx[g] = new_mx("x")
            quantise(grouped_x[g], x_mx[g])

        def quantise_xe(g):
            xe_mx[g] = new_mx("xe")
            quantise(grouped_xe[g], xe_mx[g])

        def mx_pass(out, stationary, s_cols, moving, m_cols):
            nc.tensor.matmul_mx(
                out=out,
                lhsT=stationary[0][:, s_cols].bitcast(FP8X4),
                lhsT_scale=stationary[1][:, s_cols],
                rhs=moving[0][:, m_cols].bitcast(FP8X4),
                rhs_scale=moving[1][:, m_cols],
                start=True,
                stop=True,
            )

        def block(i):
            return slice(P * i, P * (i + 1))

        def stage1_passes(g, j, pool, tag):
            bank = bank_of(pool, tag)
            for t in range(4):
                mx_pass(bank[:, block(t)], we_mx, block(t), x_mx[g], block(j))
            banks[("s1", j)] = bank

        def stage1_exit(g, j):
            if j == 0:
                grouped_xe[g] = work.tile([P, 4 * E], BF16, align_bytes=64, tag="xe", name="xe")
            cols = slice(E * j, E * (j + 1))
            nc.vector.tensor_tensor(
                out=grouped_xe[g][:, cols].rearrange("p (c t) -> p c t", t=4),
                in0=banks[("s1", j)][:].rearrange("p (t c) -> p c t", t=4),
                in1=pos_t[:, cols].rearrange("p (c t) -> p c t", t=4),
                op=ADD,
            )

        def staged_slab(o, j):
            if j % 2 == 0:
                staged[(o, j // 2)] = stage.tile([P, 2 * E], F32, name="st%d" % o, tag="st%d" % o)
            return staged[(o, j // 2)][:, E * (j % 2) : E * (j % 2 + 1)]

        def full_pass(g, j, o):
            banks[o] = bank_of(s2_pool, "s2")
            mx_pass(banks[o][:], xe_mx[g], block(j), w_mx[o], slice(0, E))

        def q_exit(j):
            nc.vector.tensor_tensor(
                out=staged_slab(Q, j), in0=banks[Q][:], in1=bias_all[:, E * Q : E * (Q + 1)], op=ADD
            )

        def k_exit(j):
            slab = staged_slab(K, j)
            nc.scalar.copy(out=slab, in_=banks[K][:])
            nc.gpsimd.tensor_tensor(
                out=slab, in0=slab, in1=bias_all[:, E * K : E * (K + 1)], op=ADD
            )

        def v_low_pass(g, j):
            if j % 2 == 0:
                banks[V] = bank_of(vlow_pool, "vlow")
                staged[(V, j // 2)] = stage.tile([P, 2 * E], F32, name="st2", tag="st2")
            mx_pass(
                banks[V][:, H * (j % 2) : H * (j % 2 + 1)], xe_mx[g], block(j), w_mx[V], slice(0, H)
            )

        def v_low_exit(pair):
            nc.vector.tensor_tensor(
                out=staged[(V, pair)][:].rearrange("c (j e) -> c j e", j=2)[:, :, 0:H],
                in0=banks[V][:].rearrange("c (j e) -> c j e", j=2),
                in1=bias_all[:, E * V : E * V + H].unsqueeze(1).to_broadcast([P, 2, H]),
                op=ADD,
            )

        def v_high_pass(g, i):
            banks[("vh", i)] = bank_of(s2_pool, "s2")
            mx_pass(banks[("vh", i)][:], w_mx[V], slice(H + P * i, H + P * (i + 1)), xe_mx[g], slice(0, E))

        def v_high_bias(i):
            v_high[i] = work.tile([P, E], F32, tag="v_high", name="v_high", bufs=4)
            nc.scalar.activation(
                out=v_high[i][:], in_=banks[("vh", i)][:], func=IDENTITY, bias=bv_col[:, i : i + 1]
            )

        def v_high_back(pair):
            bank = bank_of(prep_pool, "prep")
            for j2 in range(2):
                for i in range(2):
                    nc.tensor.transpose(
                        bank[:, block(2 * j2 + i)], v_high[i][:, block(2 * pair + j2)], ident[:]
                    )
            nc.scalar.copy(
                out=staged[(V, pair)][:].rearrange("c (j e) -> c j e", j=2)[:, :, H:E],
                in_=bank[:].rearrange("c (j e) -> c j e", j=2),
            )

        def store(g, o, pair):
            nc.sync.dma_start(
                out=outs[o][g].rearrange("(c j) h d -> c (j h d)", j=SLABS)[
                    :, 2 * E * pair : 2 * E * (pair + 1)
                ],
                in_=staged[(o, pair)][:],
            )

        grouped_we = new_grouped()
        turn_half(we_raw, grouped_we, 0, False, nc.vector.tensor_copy)
        turn_half(we_raw, grouped_we, 1, False, nc.scalar.copy)
        turn_x(0)
        be_bank = bank_of(s2_pool, "s2")
        nc.tensor.transpose(be_bank[:, 0:P], be_rows[:].bitcast(F32), ident[:])
        nc.scalar.copy(out=be_col[:], in_=be_bank[:].bitcast(BF16)[:, 0:4])
        pos_banks = [turn_words(pos_raw, 0, s2_pool, "s2"), turn_words(pos_raw, 1, vlow_pool, "vlow")]
        quantise(grouped_we, we_mx)
        quantise_x(0)
        grouped_w = {}

        def turn_weight(o):
            grouped_w[o] = new_grouped()
            for half in range(2):
                turn_half(w_raw[o], grouped_w[o], half, True, nc.scalar.copy)

        def spread_bias(o):
            bank = bank_of(s2_pool, "s2")
            cols = slice(E * o, E * (o + 1))
            nc.tensor.matmul(out=bank[:], lhsT=ones[:], rhs=bias_rows[:, cols], start=True, stop=True)
            nc.scalar.copy(out=bias_all[:, cols], in_=bank[:])

        turn_weight(K)
        for j in range(SLABS):
            if j < 2:
                stage1_passes(0, j, prep_pool, "prep")
            else:
                stage1_passes(0, j, s2_pool, "s2")
        for j in range(SLABS):
            nc.vector.tensor_tensor(
                out=pos_t[:, E * j : E * (j + 1)].rearrange("p (c u e) -> p c u e", u=2, e=2),
                in0=pos_banks[j // 2][:]
                .bitcast(BF16)
                .rearrange("p (s u c e) -> p s c u e", s=2, u=2, e=2)[:, j % 2],
                in1=be_col[:].rearrange("p (o u e) -> p o u e", o=1, u=2).to_broadcast([P, P, 2, 2]),
                op=ADD,
            )
        for j in range(SLABS):
            stage1_exit(0, j)
        turn_weight(Q)
        turn_x(1)
        turn_weight(V)
        for o in (V, Q, K):
            spread_bias(o)
        quantise(grouped_w[K], w_mx[K])
        quantise(grouped_w[Q], w_mx[Q])
        quantise_xe(0)
        quantise_x(1)
        quantise(grouped_w[V], w_mx[V])
        for j in range(2):
            stage1_passes(1, j, prep_pool, "prep")
        bv_bank = bank_of(s2_pool, "s2")
        for i in range(2):
            nc.tensor.transpose(
                bv_bank[:, block(i)], bias_all[:, E * V + H + P * i : E * V + H + P * (i + 1)], ident[:]
            )
        nc.scalar.copy(
            out=bv_col[:].unsqueeze(2),
            in_=bv_bank[:].rearrange("p (i c) -> p i c", c=P)[:, 0:2, 0:1],
        )
        for j in range(2):
            stage1_exit(1, j)

        for g in range(GROUPS):
            for j in range(SLABS):
                for o in (K, Q) if j == 0 else (Q, K):
                    full_pass(g, j, o)
                v_low_pass(g, j)
                if j == 0:
                    v_high_pass(g, 0)
                    v_high_pass(g, 1)
                if j == 0:
                    k_exit(j)
                    q_exit(j)
                elif j < 3:
                    q_exit(j)
                    k_exit(j)
                else:
                    k_exit(j)
                if j == 0:
                    v_high_bias(0)
                    v_high_bias(1)
                    if g + 1 < GROUPS:
                        stage1_passes(g + 1, 2, prep_pool, "prep")
                        stage1_passes(g + 1, 3, prep_pool, "prep")
                        stage1_exit(g + 1, 2)
                        stage1_exit(g + 1, 3)
                if j == 1:
                    v_low_exit(0)
                    if g + 2 < GROUPS:
                        turn_x(g + 2)
                    store(g, Q, 0)
                if j == 2:
                    v_high_back(0)
                    v_high_back(1)
                if j == 3:
                    store(g, K, 0)
                    store(g, V, 0)
                    if g + 2 < GROUPS:
                        quantise_x(g + 2)
                    if g + 1 < GROUPS:
                        quantise_xe(g + 1)
                    if g + 2 < GROUPS:
                        stage1_passes(g + 2, 0, prep_pool, "prep")
                        stage1_passes(g + 2, 1, prep_pool, "prep")
                    q_exit(j)
                    v_low_exit(1)
                    if g + 2 < GROUPS:
                        stage1_exit(g + 2, 0)
                        stage1_exit(g + 2, 1)
                    store(g, Q, 1)
                    store(g, V, 1)
                    store(g, K, 1)
